import numpy as np
import ml_dtypes


def mxq(x, axis, fmt="e4m3"):
    dtype, down = {"e4m3": (ml_dtypes.float8_e4m3fn, 7), "e5m2": (ml_dtypes.float8_e5m2, 14)}[fmt]
    v = np.moveaxis(np.asarray(x, np.float32).astype(ml_dtypes.bfloat16).astype(np.float64), axis, -1)
    blocks = v.reshape(v.shape[:-1] + (-1, 32))
    amax = np.abs(blocks).max(-1, keepdims=True)
    byte = np.maximum(np.where(amax > 0, np.frexp(amax)[1] - 1 + 127, 0) - down, 1)
    scale = np.exp2(byte - 127.0)
    codes = (blocks / scale).astype(np.float32).astype(dtype).astype(np.float64)
    return np.moveaxis((codes * scale).reshape(v.shape), -1, axis)


WIDE = False


def mx_kscale(k):
    if not WIDE:
        return np.ones(k)
    levels = np.array([20, -20, 10, -10, 0])
    a = np.random.permutation(np.resize(levels, k // 512 * 4)).reshape(k // 512, 4)
    idx = np.arange(k)
    return np.exp2(a[idx // 512, idx % 128 // 32])


BF16 = ml_dtypes.bfloat16


def bf(x):
    return np.asarray(x, np.float32).astype(BF16)


def f64(x):
    return np.asarray(x).astype(np.float64)


B, S, HID, NH, NOPE, ROPE, VD, KV_RANK, SW, QB = 1, 2048, 1024, 8, 64, 128, 128, 512, 384, 128
QK = NOPE + ROPE


def rotate_half(x):
    h = x.shape[-1] // 2
    return np.concatenate([-x[..., h:], x[..., :h]], axis=-1)


def rotate_half_t(y):
    h = y.shape[-1] // 2
    return np.concatenate([y[..., h:], -y[..., :h]], axis=-1)


def rope_tables():
    pos = np.arange(S, dtype=np.float64)
    inv = 1.0 / (10000.0 ** (np.arange(0, ROPE, 2, dtype=np.float64) / ROPE))
    ang = pos[:, None] * inv[None, :]
    ang = np.concatenate([ang, ang], axis=-1)
    return bf(np.broadcast_to(np.cos(ang)[None], (B, S, ROPE))), bf(np.broadcast_to(np.sin(ang)[None], (B, S, ROPE)))


def setup_inputs():
    u = np.array(mx_kscale(NH * QK), dtype=np.float64).reshape(NH, QK)
    u[:, NOPE + ROPE // 2:] = u[:, NOPE:NOPE + ROPE // 2]
    cos, sin = rope_tables()
    hs = np.random.standard_normal((B, S, HID))
    wq = np.random.standard_normal((HID, NH * QK)) * 2.0 / np.sqrt(HID) / u.reshape(-1)[None, :]
    b = np.random.standard_normal(NH * QK) * 0.2
    g = np.random.standard_normal((B, NH, S, QK)) * np.exp2(np.random.randint(-12, 1, (B, 1, S, 1))) * 4.0 * u[None, :, None, :]
    return {"hidden_states": bf(hs), "cos": cos, "sin": sin, "Wq": bf(wq), "bq": bf(b), "grad_out": bf(g)}


def reference(hidden_states, cos, sin, Wq, bq, grad_out):
    g = f64(grad_out)
    c, si = f64(cos)[:, None], f64(sin)[:, None]
    g_nope, g_rope = g[..., :NOPE], g[..., NOPE:]
    gq_rope = g_rope * c + rotate_half_t(g_rope * si)
    gq = np.concatenate([g_nope, gq_rope], axis=-1).transpose(0, 2, 1, 3).reshape(B, S, NH * QK)
    return mxq(gq, 2, "e5m2") @ mxq(f64(Wq), 1, "e4m3").T

@@ -1,0 +1,138 @@
+from contextlib import ExitStack
+
+import concourse.mybir as mybir
+from concourse.masks import make_identity
+
+BF16 = mybir.dt.bfloat16
+F32 = mybir.dt.float32
+U32 = mybir.dt.uint32
+U8 = mybir.dt.uint8
+E4M3X4 = mybir.dt.float8_e4m3fn_x4
+E5M2X4 = mybir.dt.float8_e5m2_x4
+ALU = mybir.AluOpType
+
+P = 128
+TOKENS = 2048
+HEADS = 8
+NOPE = 64
+ROPE = 128
+HALF = ROPE // 2
+HEAD = NOPE + ROPE
+K = HEADS * HEAD
+HID = 1024
+PACK = 4
+K_PASS = P * PACK
+PASSES = K // K_PASS
+N_TILE = 512
+N_HALVES = HID // N_TILE
+ROWS = 4
+CHUNK = P * ROWS
+CHUNKS = TOKENS // CHUNK
+QUADS = K // PACK
+RUN = NOPE // PACK
+
+FLOPS = 2 * TOKENS * HID * K
+BYTES = 2 * (TOKENS * K + HID * K + 2 * TOKENS * ROPE) + 4 * TOKENS * HID
+
+
+def tile_gptossmlaattention_pb_kernel(tc, hidden_states, cos, sin, Wq, bq, grad_out, out):
+    nc = tc.nc
+    with ExitStack() as pools:
+        keep = pools.enter_context(tc.tile_pool(name="keep", bufs=1))
+        stage = pools.enter_context(tc.tile_pool(name="stage", bufs=3))
+        turned = pools.enter_context(tc.psum_pool(name="turned", bufs=4))
+        sums = pools.enter_context(tc.psum_pool(name="sums", bufs=4))
+
+        ident_f32 = keep.tile([P, P], F32)
+        make_identity(nc, ident_f32[:])
+        ident_bf16 = keep.tile([P, P], BF16)
+        make_identity(nc, ident_bf16[:])
+
+        tables = keep.tile([P, 2, CHUNKS, ROWS * ROPE], BF16)
+        grads = [keep.tile([P, HEADS, ROWS * HEAD], BF16, name="grads%d" % a) for a in range(CHUNKS)]
+        w_rows = keep.tile([P, HID // P, K], BF16)
+        grad_chunks = grad_out.rearrange("b h (a p r) d -> a p (b h) (r d)", p=P, r=ROWS)
+        w_view = Wq.rearrange("(j p) k -> p j k", p=P)
+        nc.sync.dma_start(out=tables[:, 0], in_=cos.rearrange("b (a p r) d -> p (b a) (r d)", p=P, r=ROWS))
+        nc.sync.dma_start(out=tables[:, 1], in_=sin.rearrange("b (a p r) d -> p (b a) (r d)", p=P, r=ROWS))
+        nc.sync.dma_start(out=grads[0][:], in_=grad_chunks[0])
+        for pair in range(HID // P // 2):
+            nc.sync.dma_start(out=w_rows[:, 2 * pair : 2 * pair + 2, :], in_=w_view[:, 2 * pair : 2 * pair + 2, :])
+        for a in range(1, CHUNKS):
+            nc.sync.dma_start(out=grads[a][:], in_=grad_chunks[a])
+        out_rows = out.rearrange("b (a p r) n -> a r p (b n)", p=P, r=ROWS)
+
+        w_codes = keep.tile([P, PASSES, HID], U32, align_bytes=64)
+        w_scales = keep.tile([P, PASSES, HID], U8, align_bytes=64)
+        w_words = w_rows[:].bitcast(F32)
+        for half in range(N_HALVES):
+            for c in range(PASSES):
+                w_grouped = stage.tile([P, N_TILE, PACK], BF16, align_bytes=64)
+                for pair in range(2):
+                    w_turned = turned.tile([P, 2, 2 * P], F32, tag="turned")
+                    for j in range(2):
+                        for u in range(2):
+                            nc.tensor.transpose(
+                                w_turned[:, u, j * P : (j + 1) * P],
+                                w_words[:, 4 * half + 2 * pair + j, 2 * P * c + u : 2 * P * (c + 1) : 2],
+                                ident_f32[:],
+                            )
+                    nc.scalar.copy(
+                        out=w_grouped[:].bitcast(F32)[:, 2 * P * pair : 2 * P * (pair + 1), :],
+                        in_=w_turned[:].rearrange("p u n -> p n u"),
+                    )
+                cols = slice(half * N_TILE, (half + 1) * N_TILE)
+                nc.vector.quantize_mx(
+                    out=w_codes[:, c, cols].bitcast(E4M3X4),
+                    scales=w_scales[:, c, cols],
+                    in_=w_grouped[:].rearrange("p n t -> p (n t)"),
+                )
+
+        for a in range(CHUNKS):
+            for r in range(ROWS):
+                head_rows = grads[a][:, :, r * HEAD : (r + 1) * HEAD]
+                products = stage.tile([P, 2, HEADS, ROPE], F32)
+                nc.vector.tensor_tensor(
+                    out=products[:],
+                    in0=head_rows[:, :, NOPE:HEAD].unsqueeze(1).to_broadcast([P, 2, HEADS, ROPE]),
+                    in1=tables[:, :, a, r * ROPE : (r + 1) * ROPE].unsqueeze(2).to_broadcast([P, 2, HEADS, ROPE]),
+                    op=ALU.mult,
+                )
+                gq_rows = stage.tile([P, PACK, QUADS], BF16)
+                gq_parts = gq_rows[:].rearrange("p t (h c j) -> p h c j t", c=3, j=RUN)
+                split = products[:].rearrange("p x h (z j t) -> p x h z j t", z=2, t=PACK)
+                nc.scalar.copy(out=gq_parts[:, :, 0], in_=head_rows[:, :, 0:NOPE].rearrange("p h (j t) -> p h j t", t=PACK))
+                nc.vector.tensor_tensor(out=gq_parts[:, :, 1], in0=split[:, 0, :, 0], in1=split[:, 1, :, 1], op=ALU.add)
+                nc.vector.tensor_tensor(out=gq_parts[:, :, 2], in0=split[:, 0, :, 1], in1=split[:, 1, :, 0], op=ALU.subtract)
+
+                gq_grouped = stage.tile([P, PASSES, P, PACK], BF16, align_bytes=64)
+                gq_codes = stage.tile([P, PASSES, P], U32, align_bytes=64)
+                gq_scales = stage.tile([P, PASSES, P], U8, align_bytes=64)
+                for c in range(PASSES):
+                    gq_turned = turned.tile([P, PACK, P], BF16, tag="turned")
+                    for t in range(PACK):
+                        nc.tensor.transpose(gq_turned[:, t, :], gq_rows[:, t, c * P : (c + 1) * P], ident_bf16[:])
+                    nc.scalar.copy(out=gq_grouped[:, c], in_=gq_turned[:].rearrange("p t s -> p s t"))
+                for c in range(PASSES):
+                    nc.vector.quantize_mx(
+                        out=gq_codes[:, c, :].bitcast(E5M2X4),
+                        scales=gq_scales[:, c, :],
+                        in_=gq_grouped[:, c].rearrange("p s t -> p (s t)"),
+                    )
+
+                result = stage.tile([P, HID], F32)
+                for half in range(N_HALVES):
+                    cols = slice(half * N_TILE, (half + 1) * N_TILE)
+                    acc = sums.tile([P, N_TILE], F32)
+                    for c in range(PASSES):
+                        nc.tensor.matmul_mx(
+                            out=acc[:],
+                            lhsT=gq_codes[:, c, :].bitcast(E5M2X4),
+                            lhsT_scale=gq_scales[:, c, :],
+                            rhs=w_codes[:, c, cols].bitcast(E4M3X4),
+                            rhs_scale=w_scales[:, c, cols],
+                            start=(c == 0),
+                            stop=(c == PASSES - 1),
+                        )
+                    nc.scalar.copy(out=result[:, cols], in_=acc[:])
+                nc.sync.dma_start(out=out_rows[a][r], in_=result[:])

@@ -40,8 +40,9 @@ def tile_gptossmlaattention_pb_kernel(tc, hidden_states, cos, sin, Wq, bq, grad_
     with ExitStack() as pools:
         keep = pools.enter_context(tc.tile_pool(name="keep", bufs=1))
         stage = pools.enter_context(tc.tile_pool(name="stage", bufs=3))
-        turned = pools.enter_context(tc.psum_pool(name="turned", bufs=4))
+        turned = pools.enter_context(tc.psum_pool(name="turned", bufs=3))
         sums = pools.enter_context(tc.psum_pool(name="sums", bufs=4))
+        angles = pools.enter_context(tc.psum_pool(name="angles", bufs=1))
 
         ident_f32 = keep.tile([P, P], F32)
         make_identity(nc, ident_f32[:])
@@ -53,11 +54,14 @@ def tile_gptossmlaattention_pb_kernel(tc, hidden_states, cos, sin, Wq, bq, grad_
         w_rows = keep.tile([P, HID // P, K], BF16)
         grad_chunks = grad_out.rearrange("b h (a p r) d -> a p (b h) (r d)", p=P, r=ROWS)
         w_view = Wq.rearrange("(j p) k -> p j k", p=P)
-        nc.sync.dma_start(out=tables[:, 0], in_=cos.rearrange("b (a p r) d -> p (b a) (r d)", p=P, r=ROWS))
-        nc.sync.dma_start(out=tables[:, 1], in_=sin.rearrange("b (a p r) d -> p (b a) (r d)", p=P, r=ROWS))
+        table_views = [x.rearrange("b (a p r) d -> p (b a) (r d)", p=P, r=ROWS) for x in (cos, sin)]
+        for x in range(2):
+            nc.sync.dma_start(out=tables[:, x, 0:1], in_=table_views[x][:, 0:1])
         nc.sync.dma_start(out=grads[0][:], in_=grad_chunks[0])
         for pair in range(HID // P // 2):
             nc.sync.dma_start(out=w_rows[:, 2 * pair : 2 * pair + 2, :], in_=w_view[:, 2 * pair : 2 * pair + 2, :])
+        for x in range(2):
+            nc.sync.dma_start(out=tables[:, x, 1:CHUNKS], in_=table_views[x][:, 1:CHUNKS])
         for a in range(1, CHUNKS):
             nc.sync.dma_start(out=grads[a][:], in_=grad_chunks[a])
         out_rows = out.rearrange("b (a p r) n -> a r p (b n)", p=P, r=ROWS)
@@ -89,21 +93,24 @@ def tile_gptossmlaattention_pb_kernel(tc, hidden_states, cos, sin, Wq, bq, grad_
                 )
 
         for a in range(CHUNKS):
+            angle_rows = angles.tile([P, 2, ROWS * ROPE], BF16)
+            for x in range(2):
+                nc.tensor.matmul(out=angle_rows[:, x, :], lhsT=ident_bf16[:], rhs=tables[:, x, a, :], start=True, stop=True)
             for r in range(ROWS):
                 head_rows = grads[a][:, :, r * HEAD : (r + 1) * HEAD]
                 products = stage.tile([P, 2, HEADS, ROPE], F32)
                 nc.vector.tensor_tensor(
                     out=products[:],
                     in0=head_rows[:, :, NOPE:HEAD].unsqueeze(1).to_broadcast([P, 2, HEADS, ROPE]),
-                    in1=tables[:, :, a, r * ROPE : (r + 1) * ROPE].unsqueeze(2).to_broadcast([P, 2, HEADS, ROPE]),
+                    in1=angle_rows[:, :, r * ROPE : (r + 1) * ROPE].unsqueeze(2).to_broadcast([P, 2, HEADS, ROPE]),
                     op=ALU.mult,
                 )
                 gq_rows = stage.tile([P, PACK, QUADS], BF16)
                 gq_parts = gq_rows[:].rearrange("p t (h c j) -> p h c j t", c=3, j=RUN)
                 split = products[:].rearrange("p x h (z j t) -> p x h z j t", z=2, t=PACK)
                 nc.scalar.copy(out=gq_parts[:, :, 0], in_=head_rows[:, :, 0:NOPE].rearrange("p h (j t) -> p h j t", t=PACK))
-                nc.vector.tensor_tensor(out=gq_parts[:, :, 1], in0=split[:, 0, :, 0], in1=split[:, 1, :, 1], op=ALU.add)
-                nc.vector.tensor_tensor(out=gq_parts[:, :, 2], in0=split[:, 0, :, 1], in1=split[:, 1, :, 0], op=ALU.subtract)
+                nc.gpsimd.tensor_tensor(out=gq_parts[:, :, 1], in0=split[:, 0, :, 0], in1=split[:, 1, :, 1], op=ALU.add)
+                nc.gpsimd.tensor_tensor(out=gq_parts[:, :, 2], in0=split[:, 0, :, 1], in1=split[:, 1, :, 0], op=ALU.subtract)
 
                 gq_grouped = stage.tile([P, PASSES, P, PACK], BF16, align_bytes=64)
                 gq_codes = stage.tile([P, PASSES, P], U32, align_bytes=64)
@@ -134,5 +141,8 @@ def tile_gptossmlaattention_pb_kernel(tc, hidden_states, cos, sin, Wq, bq, grad_
                             start=(c == 0),
                             stop=(c == PASSES - 1),
                         )
-                    nc.scalar.copy(out=result[:, cols], in_=acc[:])
+                    if half == 0:
+                        nc.scalar.copy(out=result[:, cols], in_=acc[:])
+                    else:
+                        nc.vector.tensor_copy(out=result[:, cols], in_=acc[:])
                 nc.sync.dma_start(out=out_rows[a][r], in_=result[:])

@@ -28,26 +28,38 @@ N_HALVES = HID // N_TILE
 ROWS = 4
 CHUNK = P * ROWS
 CHUNKS = TOKENS // CHUNK
-QUADS = K // PACK
-RUN = NOPE // PACK
+PAIR = 2
+WORDS = K_PASS // 2
 
 FLOPS = 2 * TOKENS * HID * K
 BYTES = 2 * (TOKENS * K + HID * K + 2 * TOKENS * ROPE) + 4 * TOKENS * HID
+
+
+def turn_and_quantise(nc, turned, stage, ident, row_words, c, codes, scales, fmt):
+    bank = turned.tile([P, 2, PAIR * P], F32, tag="turned")
+    for i in range(PAIR):
+        for u in range(2):
+            nc.tensor.transpose(
+                bank[:, u, i * P : (i + 1) * P],
+                row_words[i][:, WORDS * c + u : WORDS * (c + 1) : 2],
+                ident[:],
+            )
+    grouped = stage.tile([P, PAIR * P, PACK], BF16, align_bytes=64, tag="grouped")
+    nc.scalar.copy(out=grouped[:].bitcast(F32), in_=bank[:].rearrange("p u n -> p n u"))
+    nc.vector.quantize_mx(out=codes.bitcast(fmt), scales=scales, in_=grouped[:].rearrange("p n t -> p (n t)"))
 
 
 def tile_gptossmlaattention_pb_kernel(tc, hidden_states, cos, sin, Wq, bq, grad_out, out):
     nc = tc.nc
     with ExitStack() as pools:
         keep = pools.enter_context(tc.tile_pool(name="keep", bufs=1))
+        wide = pools.enter_context(tc.tile_pool(name="wide", bufs=2))
         stage = pools.enter_context(tc.tile_pool(name="stage", bufs=3))
-        turned = pools.enter_context(tc.psum_pool(name="turned", bufs=3))
+        turned = pools.enter_context(tc.psum_pool(name="turned", bufs=4))
         sums = pools.enter_context(tc.psum_pool(name="sums", bufs=4))
-        angles = pools.enter_context(tc.psum_pool(name="angles", bufs=1))
 
-        ident_f32 = keep.tile([P, P], F32)
-        make_identity(nc, ident_f32[:])
-        ident_bf16 = keep.tile([P, P], BF16)
-        make_identity(nc, ident_bf16[:])
+        ident = keep.tile([P, P], F32)
+        make_identity(nc, ident[:])
 
         tables = keep.tile([P, 2, CHUNKS, ROWS * ROPE], BF16)
         grads = [keep.tile([P, HEADS, ROWS * HEAD], BF16, name="grads%d" % a) for a in range(CHUNKS)]
@@ -58,91 +70,83 @@ def tile_gptossmlaattention_pb_kernel(tc, hidden_states, cos, sin, Wq, bq, grad_
         for x in range(2):
             nc.sync.dma_start(out=tables[:, x, 0:1], in_=table_views[x][:, 0:1])
         nc.sync.dma_start(out=grads[0][:], in_=grad_chunks[0])
-        for pair in range(HID // P // 2):
-            nc.sync.dma_start(out=w_rows[:, 2 * pair : 2 * pair + 2, :], in_=w_view[:, 2 * pair : 2 * pair + 2, :])
+        for q in range(HID // P // PAIR):
+            nc.sync.dma_start(out=w_rows[:, PAIR * q : PAIR * (q + 1), :], in_=w_view[:, PAIR * q : PAIR * (q + 1), :])
         for x in range(2):
             nc.sync.dma_start(out=tables[:, x, 1:CHUNKS], in_=table_views[x][:, 1:CHUNKS])
         for a in range(1, CHUNKS):
             nc.sync.dma_start(out=grads[a][:], in_=grad_chunks[a])
-        out_rows = out.rearrange("b (a p r) n -> a r p (b n)", p=P, r=ROWS)
+        out_rows = out.rearrange("b (a p r) n -> a p (b r) n", p=P, r=ROWS)
 
         w_codes = keep.tile([P, PASSES, HID], U32, align_bytes=64)
         w_scales = keep.tile([P, PASSES, HID], U8, align_bytes=64)
         w_words = w_rows[:].bitcast(F32)
-        for half in range(N_HALVES):
+        for q in range(HID // P // PAIR):
+            cols = slice(PAIR * P * q, PAIR * P * (q + 1))
             for c in range(PASSES):
-                w_grouped = stage.tile([P, N_TILE, PACK], BF16, align_bytes=64)
-                for pair in range(2):
-                    w_turned = turned.tile([P, 2, 2 * P], F32, tag="turned")
-                    for j in range(2):
-                        for u in range(2):
-                            nc.tensor.transpose(
-                                w_turned[:, u, j * P : (j + 1) * P],
-                                w_words[:, 4 * half + 2 * pair + j, 2 * P * c + u : 2 * P * (c + 1) : 2],
-                                ident_f32[:],
-                            )
-                    nc.scalar.copy(
-                        out=w_grouped[:].bitcast(F32)[:, 2 * P * pair : 2 * P * (pair + 1), :],
-                        in_=w_turned[:].rearrange("p u n -> p n u"),
-                    )
-                cols = slice(half * N_TILE, (half + 1) * N_TILE)
-                nc.vector.quantize_mx(
-                    out=w_codes[:, c, cols].bitcast(E4M3X4),
-                    scales=w_scales[:, c, cols],
-                    in_=w_grouped[:].rearrange("p n t -> p (n t)"),
+                turn_and_quantise(
+                    nc, turned, stage, ident, [w_words[:, PAIR * q + i, :] for i in range(PAIR)], c,
+                    w_codes[:, c, cols], w_scales[:, c, cols], E4M3X4,
                 )
 
         for a in range(CHUNKS):
-            angle_rows = angles.tile([P, 2, ROWS * ROPE], BF16)
-            for x in range(2):
-                nc.tensor.matmul(out=angle_rows[:, x, :], lhsT=ident_bf16[:], rhs=tables[:, x, a, :], start=True, stop=True)
-            for r in range(ROWS):
-                head_rows = grads[a][:, :, r * HEAD : (r + 1) * HEAD]
-                products = stage.tile([P, 2, HEADS, ROPE], F32)
-                nc.vector.tensor_tensor(
-                    out=products[:],
-                    in0=head_rows[:, :, NOPE:HEAD].unsqueeze(1).to_broadcast([P, 2, HEADS, ROPE]),
-                    in1=angle_rows[:, :, r * ROPE : (r + 1) * ROPE].unsqueeze(2).to_broadcast([P, 2, HEADS, ROPE]),
-                    op=ALU.mult,
+            by_token = grads[a][:].rearrange("p h (r d) -> p r h d", r=ROWS)
+            by_token_words = grads[a][:].bitcast(F32).rearrange("p h (r w) -> p r h w", r=ROWS)
+            for r0 in range(0, ROWS, PAIR):
+                products = wide.tile([P, 2, PAIR, HEADS, ROPE], F32)
+                for x in range(2):
+                    nc.vector.tensor_tensor(
+                        out=products[:, x],
+                        in0=by_token[:, r0 : r0 + PAIR, :, NOPE:HEAD],
+                        in1=tables[:, x, a, r0 * ROPE : (r0 + PAIR) * ROPE]
+                        .rearrange("p (r d) -> p r d", r=PAIR)
+                        .unsqueeze(2)
+                        .to_broadcast([P, PAIR, HEADS, ROPE]),
+                        op=ALU.mult,
+                    )
+                gq_rows = stage.tile([P, PAIR, K], BF16)
+                gq_heads = gq_rows[:].rearrange("p r (h d) -> p r h d", h=HEADS)
+                nc.scalar.copy(
+                    out=gq_rows[:].bitcast(F32).rearrange("p r (h w) -> p r h w", h=HEADS)[:, :, :, 0 : NOPE // 2],
+                    in_=by_token_words[:, r0 : r0 + PAIR, :, 0 : NOPE // 2],
                 )
-                gq_rows = stage.tile([P, PACK, QUADS], BF16)
-                gq_parts = gq_rows[:].rearrange("p t (h c j) -> p h c j t", c=3, j=RUN)
-                split = products[:].rearrange("p x h (z j t) -> p x h z j t", z=2, t=PACK)
-                nc.scalar.copy(out=gq_parts[:, :, 0], in_=head_rows[:, :, 0:NOPE].rearrange("p h (j t) -> p h j t", t=PACK))
-                nc.gpsimd.tensor_tensor(out=gq_parts[:, :, 1], in0=split[:, 0, :, 0], in1=split[:, 1, :, 1], op=ALU.add)
-                nc.gpsimd.tensor_tensor(out=gq_parts[:, :, 2], in0=split[:, 0, :, 1], in1=split[:, 1, :, 0], op=ALU.subtract)
+                nc.vector.tensor_tensor(
+                    out=gq_heads[:, :, :, NOPE : NOPE + HALF],
+                    in0=products[:, 0, :, :, 0:HALF],
+                    in1=products[:, 1, :, :, HALF:ROPE],
+                    op=ALU.add,
+                )
+                nc.vector.tensor_tensor(
+                    out=gq_heads[:, :, :, NOPE + HALF : HEAD],
+                    in0=products[:, 0, :, :, HALF:ROPE],
+                    in1=products[:, 1, :, :, 0:HALF],
+                    op=ALU.subtract,
+                )
 
-                gq_grouped = stage.tile([P, PASSES, P, PACK], BF16, align_bytes=64)
-                gq_codes = stage.tile([P, PASSES, P], U32, align_bytes=64)
-                gq_scales = stage.tile([P, PASSES, P], U8, align_bytes=64)
+                gq_codes = stage.tile([P, PASSES, PAIR * P], U32, align_bytes=64)
+                gq_scales = stage.tile([P, PASSES, PAIR * P], U8, align_bytes=64)
+                gq_words = gq_rows[:].bitcast(F32)
                 for c in range(PASSES):
-                    gq_turned = turned.tile([P, PACK, P], BF16, tag="turned")
-                    for t in range(PACK):
-                        nc.tensor.transpose(gq_turned[:, t, :], gq_rows[:, t, c * P : (c + 1) * P], ident_bf16[:])
-                    nc.scalar.copy(out=gq_grouped[:, c], in_=gq_turned[:].rearrange("p t s -> p s t"))
-                for c in range(PASSES):
-                    nc.vector.quantize_mx(
-                        out=gq_codes[:, c, :].bitcast(E5M2X4),
-                        scales=gq_scales[:, c, :],
-                        in_=gq_grouped[:, c].rearrange("p s t -> p (s t)"),
+                    turn_and_quantise(
+                        nc, turned, stage, ident, [gq_words[:, i, :] for i in range(PAIR)], c,
+                        gq_codes[:, c, :], gq_scales[:, c, :], E5M2X4,
                     )
 
-                result = stage.tile([P, HID], F32)
-                for half in range(N_HALVES):
-                    cols = slice(half * N_TILE, (half + 1) * N_TILE)
-                    acc = sums.tile([P, N_TILE], F32)
-                    for c in range(PASSES):
-                        nc.tensor.matmul_mx(
-                            out=acc[:],
-                            lhsT=gq_codes[:, c, :].bitcast(E5M2X4),
-                            lhsT_scale=gq_scales[:, c, :],
-                            rhs=w_codes[:, c, cols].bitcast(E4M3X4),
-                            rhs_scale=w_scales[:, c, cols],
-                            start=(c == 0),
-                            stop=(c == PASSES - 1),
-                        )
-                    if half == 0:
-                        nc.scalar.copy(out=result[:, cols], in_=acc[:])
-                    else:
-                        nc.vector.tensor_copy(out=result[:, cols], in_=acc[:])
-                nc.sync.dma_start(out=out_rows[a][r], in_=result[:])
+                result = stage.tile([P, PAIR, HID], F32)
+                for i in range(PAIR):
+                    rows = slice(i * P, (i + 1) * P)
+                    for half in range(N_HALVES):
+                        cols = slice(half * N_TILE, (half + 1) * N_TILE)
+                        acc = sums.tile([P, N_TILE], F32)
+                        for c in range(PASSES):
+                            nc.tensor.matmul_mx(
+                                out=acc[:],
+                                lhsT=gq_codes[:, c, rows].bitcast(E5M2X4),
+                                lhsT_scale=gq_scales[:, c, rows],
+                                rhs=w_codes[:, c, cols].bitcast(E4M3X4),
+                                rhs_scale=w_scales[:, c, cols],
+                                start=(c == 0),
+                                stop=(c == PASSES - 1),
+                            )
+                        nc.scalar.copy(out=result[:, i, cols], in_=acc[:])
+                nc.sync.dma_start(out=out_rows[a][:, r0 : r0 + PAIR, :], in_=result[:])

@@ -55,11 +55,14 @@ def tile_gptossmlaattention_pb_kernel(tc, hidden_states, cos, sin, Wq, bq, grad_
         keep = pools.enter_context(tc.tile_pool(name="keep", bufs=1))
         wide = pools.enter_context(tc.tile_pool(name="wide", bufs=2))
         stage = pools.enter_context(tc.tile_pool(name="stage", bufs=3))
-        turned = pools.enter_context(tc.psum_pool(name="turned", bufs=4))
+        turned = pools.enter_context(tc.psum_pool(name="turned", bufs=3))
         sums = pools.enter_context(tc.psum_pool(name="sums", bufs=4))
+        angles = pools.enter_context(tc.psum_pool(name="angles", bufs=1))
 
         ident = keep.tile([P, P], F32)
         make_identity(nc, ident[:])
+        ident_bf16 = keep.tile([P, P], BF16)
+        make_identity(nc, ident_bf16[:])
 
         tables = keep.tile([P, 2, CHUNKS, ROWS * ROPE], BF16)
         grads = [keep.tile([P, HEADS, ROWS * HEAD], BF16, name="grads%d" % a) for a in range(CHUNKS)]
@@ -92,13 +95,16 @@ def tile_gptossmlaattention_pb_kernel(tc, hidden_states, cos, sin, Wq, bq, grad_
         for a in range(CHUNKS):
             by_token = grads[a][:].rearrange("p h (r d) -> p r h d", r=ROWS)
             by_token_words = grads[a][:].bitcast(F32).rearrange("p h (r w) -> p r h w", r=ROWS)
+            angle_rows = angles.tile([P, 2, ROWS * ROPE], BF16)
+            for x in range(2):
+                nc.tensor.matmul(out=angle_rows[:, x, :], lhsT=ident_bf16[:], rhs=tables[:, x, a, :], start=True, stop=True)
             for r0 in range(0, ROWS, PAIR):
                 products = wide.tile([P, 2, PAIR, HEADS, ROPE], F32)
                 for x in range(2):
                     nc.vector.tensor_tensor(
                         out=products[:, x],
                         in0=by_token[:, r0 : r0 + PAIR, :, NOPE:HEAD],
-                        in1=tables[:, x, a, r0 * ROPE : (r0 + PAIR) * ROPE]
+                        in1=angle_rows[:, x, r0 * ROPE : (r0 + PAIR) * ROPE]
                         .rearrange("p (r d) -> p r d", r=PAIR)
                         .unsqueeze(2)
                         .to_broadcast([P, PAIR, HEADS, ROPE]),
@@ -110,13 +116,13 @@ def tile_gptossmlaattention_pb_kernel(tc, hidden_states, cos, sin, Wq, bq, grad_
                     out=gq_rows[:].bitcast(F32).rearrange("p r (h w) -> p r h w", h=HEADS)[:, :, :, 0 : NOPE // 2],
                     in_=by_token_words[:, r0 : r0 + PAIR, :, 0 : NOPE // 2],
                 )
-                nc.vector.tensor_tensor(
+                nc.gpsimd.tensor_tensor(
                     out=gq_heads[:, :, :, NOPE : NOPE + HALF],
                     in0=products[:, 0, :, :, 0:HALF],
                     in1=products[:, 1, :, :, HALF:ROPE],
                     op=ALU.add,
                 )
-                nc.vector.tensor_tensor(
+                nc.gpsimd.tensor_tensor(
                     out=gq_heads[:, :, :, NOPE + HALF : HEAD],
                     in0=products[:, 0, :, :, HALF:ROPE],
                     in1=products[:, 1, :, :, 0:HALF],

@@ -25,134 +25,168 @@ K_PASS = P * PACK
 PASSES = K // K_PASS
 N_TILE = 512
 N_HALVES = HID // N_TILE
-ROWS = 4
-CHUNK = P * ROWS
-CHUNKS = TOKENS // CHUNK
 PAIR = 2
+CHUNK = P * PAIR
+CHUNKS = TOKENS // CHUNK
 WORDS = K_PASS // 2
 
 FLOPS = 2 * TOKENS * HID * K
 BYTES = 2 * (TOKENS * K + HID * K + 2 * TOKENS * ROPE) + 4 * TOKENS * HID
 
 
-def turn_and_quantise(nc, turned, stage, ident, row_words, c, codes, scales, fmt):
-    bank = turned.tile([P, 2, PAIR * P], F32, tag="turned")
-    for i in range(PAIR):
-        for u in range(2):
-            nc.tensor.transpose(
-                bank[:, u, i * P : (i + 1) * P],
-                row_words[i][:, WORDS * c + u : WORDS * (c + 1) : 2],
-                ident[:],
-            )
-    grouped = stage.tile([P, PAIR * P, PACK], BF16, align_bytes=64, tag="grouped")
-    nc.scalar.copy(out=grouped[:].bitcast(F32), in_=bank[:].rearrange("p u n -> p n u"))
-    nc.vector.quantize_mx(out=codes.bitcast(fmt), scales=scales, in_=grouped[:].rearrange("p n t -> p (n t)"))
-
-
 def tile_gptossmlaattention_pb_kernel(tc, hidden_states, cos, sin, Wq, bq, grad_out, out):
     nc = tc.nc
-    with ExitStack() as pools:
-        keep = pools.enter_context(tc.tile_pool(name="keep", bufs=1))
-        wide = pools.enter_context(tc.tile_pool(name="wide", bufs=2))
-        stage = pools.enter_context(tc.tile_pool(name="stage", bufs=3))
-        turned = pools.enter_context(tc.psum_pool(name="turned", bufs=3))
-        sums = pools.enter_context(tc.psum_pool(name="sums", bufs=4))
-        angles = pools.enter_context(tc.psum_pool(name="angles", bufs=1))
+    with ExitStack() as ctx:
+        keep = ctx.enter_context(tc.tile_pool(name="keep", bufs=1))
+        stage = ctx.enter_context(tc.tile_pool(name="stage", bufs=2))
+        results = ctx.enter_context(tc.tile_pool(name="results", bufs=3))
+        turned = ctx.enter_context(tc.psum_pool(name="turned", bufs=4))
+        sums = ctx.enter_context(tc.psum_pool(name="sums", bufs=4))
+        ctx.enter_context(tc.manual_schedule())
 
         ident = keep.tile([P, P], F32)
         make_identity(nc, ident[:])
-        ident_bf16 = keep.tile([P, P], BF16)
-        make_identity(nc, ident_bf16[:])
 
-        tables = keep.tile([P, 2, CHUNKS, ROWS * ROPE], BF16)
-        grads = [keep.tile([P, HEADS, ROWS * HEAD], BF16, name="grads%d" % a) for a in range(CHUNKS)]
+        tables = keep.tile([P, 2, CHUNKS, PAIR * ROPE], BF16)
+        grads = [keep.tile([P, HEADS, PAIR * HEAD], BF16, name="grads%d" % a) for a in range(CHUNKS)]
         w_rows = keep.tile([P, HID // P, K], BF16)
-        grad_chunks = grad_out.rearrange("b h (a p r) d -> a p (b h) (r d)", p=P, r=ROWS)
+        grad_chunks = grad_out.rearrange("b h (a p r) d -> a p (b h) (r d)", p=P, r=PAIR)
+        table_views = [x.rearrange("b (a p r) d -> p (b a) (r d)", p=P, r=PAIR) for x in (cos, sin)]
         w_view = Wq.rearrange("(j p) k -> p j k", p=P)
-        table_views = [x.rearrange("b (a p r) d -> p (b a) (r d)", p=P, r=ROWS) for x in (cos, sin)]
+        out_rows = out.rearrange("b (a p r) n -> a p (b r) n", p=P, r=PAIR)
         for x in range(2):
-            nc.sync.dma_start(out=tables[:, x, 0:1], in_=table_views[x][:, 0:1])
-        nc.sync.dma_start(out=grads[0][:], in_=grad_chunks[0])
+            nc.sync.dma_start(out=tables[:, x, 0:2], in_=table_views[x][:, 0:2])
+        for a in range(2):
+            nc.sync.dma_start(out=grads[a][:], in_=grad_chunks[a])
         for q in range(HID // P // PAIR):
             nc.sync.dma_start(out=w_rows[:, PAIR * q : PAIR * (q + 1), :], in_=w_view[:, PAIR * q : PAIR * (q + 1), :])
         for x in range(2):
-            nc.sync.dma_start(out=tables[:, x, 1:CHUNKS], in_=table_views[x][:, 1:CHUNKS])
-        for a in range(1, CHUNKS):
+            nc.sync.dma_start(out=tables[:, x, 2:CHUNKS], in_=table_views[x][:, 2:CHUNKS])
+        for a in range(2, CHUNKS):
             nc.sync.dma_start(out=grads[a][:], in_=grad_chunks[a])
-        out_rows = out.rearrange("b (a p r) n -> a p (b r) n", p=P, r=ROWS)
 
+        def turn(row_words, c, grouped):
+            n = len(row_words)
+            bank = turned.tile([P, 2, n * P], F32, tag="turned")
+            for i in range(n):
+                for u in range(2):
+                    nc.tensor.transpose(
+                        bank[:, u, i * P : (i + 1) * P],
+                        row_words[i][:, WORDS * c + u : WORDS * (c + 1) : 2],
+                        ident[:],
+                    )
+            nc.scalar.copy(out=grouped.bitcast(F32), in_=bank[:].rearrange("p u n -> p n u"))
+
+        def products_of(a, r0, n):
+            products = stage.tile([P, 2, PAIR, HEADS, ROPE], F32)
+            by_token = grads[a][:].rearrange("p h (r d) -> p r h d", r=PAIR)
+            for x in range(2):
+                nc.vector.tensor_tensor(
+                    out=products[:, x, 0:n],
+                    in0=by_token[:, r0 : r0 + n, :, NOPE:HEAD],
+                    in1=tables[:, x, a, r0 * ROPE : (r0 + n) * ROPE]
+                    .rearrange("p (r d) -> p r d", r=n)
+                    .unsqueeze(2)
+                    .to_broadcast([P, n, HEADS, ROPE]),
+                    op=ALU.mult,
+                )
+            return products
+
+        def unrotated_of(a, r0, n):
+            gq_rows = stage.tile([P, PAIR, K], BF16)
+            by_token_words = grads[a][:].bitcast(F32).rearrange("p h (r w) -> p r h w", r=PAIR)
+            nc.scalar.copy(
+                out=gq_rows[:].bitcast(F32).rearrange("p r (h w) -> p r h w", h=HEADS)[:, 0:n, :, 0 : NOPE // 2],
+                in_=by_token_words[:, r0 : r0 + n, :, 0 : NOPE // 2],
+            )
+            return gq_rows
+
+        def add_halves(n, products, gq_rows):
+            gq_heads = gq_rows[:].rearrange("p r (h d) -> p r h d", h=HEADS)
+            nc.vector.tensor_tensor(
+                out=gq_heads[:, 0:n, :, NOPE : NOPE + HALF],
+                in0=products[:, 0, 0:n, :, 0:HALF],
+                in1=products[:, 1, 0:n, :, HALF:ROPE],
+                op=ALU.add,
+            )
+            nc.vector.tensor_tensor(
+                out=gq_heads[:, 0:n, :, NOPE + HALF : HEAD],
+                in0=products[:, 0, 0:n, :, HALF:ROPE],
+                in1=products[:, 1, 0:n, :, 0:HALF],
+                op=ALU.subtract,
+            )
+
+        def turn_tokens(n, gq_rows):
+            gq_grouped = stage.tile([P, PASSES, PAIR * P, PACK], BF16, align_bytes=64)
+            gq_words = gq_rows[:].bitcast(F32)
+            for c in range(PASSES):
+                turn([gq_words[:, i, :] for i in range(n)], c, gq_grouped[:, c, 0 : n * P, :])
+            return gq_grouped
+
+        def quantise_tokens(n, gq_grouped):
+            gq_codes = stage.tile([P, PASSES, PAIR * P], U32, align_bytes=64)
+            gq_scales = stage.tile([P, PASSES, PAIR * P], U8, align_bytes=64)
+            for c in range(PASSES):
+                nc.vector.quantize_mx(
+                    out=gq_codes[:, c, 0 : n * P].bitcast(E5M2X4),
+                    scales=gq_scales[:, c, 0 : n * P],
+                    in_=gq_grouped[:, c, 0 : n * P, :].rearrange("p s t -> p (s t)"),
+                )
+            return gq_codes, gq_scales
+
+        def multiply(a, r0, n, gq_codes, gq_scales):
+            result = results.tile([P, PAIR, HID], F32)
+            for i in range(n):
+                rows = slice(i * P, (i + 1) * P)
+                for half in range(N_HALVES):
+                    cols = slice(half * N_TILE, (half + 1) * N_TILE)
+                    acc = sums.tile([P, N_TILE], F32)
+                    for c in range(PASSES):
+                        nc.tensor.matmul_mx(
+                            out=acc[:],
+                            lhsT=gq_codes[:, c, rows].bitcast(E5M2X4),
+                            lhsT_scale=gq_scales[:, c, rows],
+                            rhs=w_codes[:, c, cols].bitcast(E4M3X4),
+                            rhs_scale=w_scales[:, c, cols],
+                            start=(c == 0),
+                            stop=(c == PASSES - 1),
+                        )
+                    nc.scalar.copy(out=result[:, i, cols], in_=acc[:])
+            nc.sync.dma_start(out=out_rows[a][:, r0 : r0 + n, :], in_=result[:, 0:n, :])
+
+        units = [(a, 0, PAIR) for a in range(CHUNKS - 1)] + [(CHUNKS - 1, r, 1) for r in range(PAIR)]
+
+        w_grouped = keep.tile([P, PASSES, HID, PACK], BF16, align_bytes=64)
         w_codes = keep.tile([P, PASSES, HID], U32, align_bytes=64)
         w_scales = keep.tile([P, PASSES, HID], U8, align_bytes=64)
         w_words = w_rows[:].bitcast(F32)
-        for q in range(HID // P // PAIR):
-            cols = slice(PAIR * P * q, PAIR * P * (q + 1))
-            for c in range(PASSES):
-                turn_and_quantise(
-                    nc, turned, stage, ident, [w_words[:, PAIR * q + i, :] for i in range(PAIR)], c,
-                    w_codes[:, c, cols], w_scales[:, c, cols], E4M3X4,
-                )
 
-        for a in range(CHUNKS):
-            by_token = grads[a][:].rearrange("p h (r d) -> p r h d", r=ROWS)
-            by_token_words = grads[a][:].bitcast(F32).rearrange("p h (r w) -> p r h w", r=ROWS)
-            angle_rows = angles.tile([P, 2, ROWS * ROPE], BF16)
-            for x in range(2):
-                nc.tensor.matmul(out=angle_rows[:, x, :], lhsT=ident_bf16[:], rhs=tables[:, x, a, :], start=True, stop=True)
-            for r0 in range(0, ROWS, PAIR):
-                products = wide.tile([P, 2, PAIR, HEADS, ROPE], F32)
-                for x in range(2):
-                    nc.vector.tensor_tensor(
-                        out=products[:, x],
-                        in0=by_token[:, r0 : r0 + PAIR, :, NOPE:HEAD],
-                        in1=angle_rows[:, x, r0 * ROPE : (r0 + PAIR) * ROPE]
-                        .rearrange("p (r d) -> p r d", r=PAIR)
-                        .unsqueeze(2)
-                        .to_broadcast([P, PAIR, HEADS, ROPE]),
-                        op=ALU.mult,
-                    )
-                gq_rows = stage.tile([P, PAIR, K], BF16)
-                gq_heads = gq_rows[:].rearrange("p r (h d) -> p r h d", h=HEADS)
-                nc.scalar.copy(
-                    out=gq_rows[:].bitcast(F32).rearrange("p r (h w) -> p r h w", h=HEADS)[:, :, :, 0 : NOPE // 2],
-                    in_=by_token_words[:, r0 : r0 + PAIR, :, 0 : NOPE // 2],
-                )
-                nc.gpsimd.tensor_tensor(
-                    out=gq_heads[:, :, :, NOPE : NOPE + HALF],
-                    in0=products[:, 0, :, :, 0:HALF],
-                    in1=products[:, 1, :, :, HALF:ROPE],
-                    op=ALU.add,
-                )
-                nc.gpsimd.tensor_tensor(
-                    out=gq_heads[:, :, :, NOPE + HALF : HEAD],
-                    in0=products[:, 0, :, :, HALF:ROPE],
-                    in1=products[:, 1, :, :, 0:HALF],
-                    op=ALU.subtract,
-                )
-
-                gq_codes = stage.tile([P, PASSES, PAIR * P], U32, align_bytes=64)
-                gq_scales = stage.tile([P, PASSES, PAIR * P], U8, align_bytes=64)
-                gq_words = gq_rows[:].bitcast(F32)
+        before = None
+        for i, (a, r0, n) in enumerate(units):
+            products = products_of(a, r0, n)
+            gq_rows = unrotated_of(a, r0, n)
+            if i == 1:
                 for c in range(PASSES):
-                    turn_and_quantise(
-                        nc, turned, stage, ident, [gq_words[:, i, :] for i in range(PAIR)], c,
-                        gq_codes[:, c, :], gq_scales[:, c, :], E5M2X4,
+                    nc.vector.quantize_mx(
+                        out=w_codes[:, c, :].bitcast(E4M3X4),
+                        scales=w_scales[:, c, :],
+                        in_=w_grouped[:, c].rearrange("p n t -> p (n t)"),
                     )
-
-                result = stage.tile([P, PAIR, HID], F32)
-                for i in range(PAIR):
-                    rows = slice(i * P, (i + 1) * P)
-                    for half in range(N_HALVES):
-                        cols = slice(half * N_TILE, (half + 1) * N_TILE)
-                        acc = sums.tile([P, N_TILE], F32)
-                        for c in range(PASSES):
-                            nc.tensor.matmul_mx(
-                                out=acc[:],
-                                lhsT=gq_codes[:, c, rows].bitcast(E5M2X4),
-                                lhsT_scale=gq_scales[:, c, rows],
-                                rhs=w_codes[:, c, cols].bitcast(E4M3X4),
-                                rhs_scale=w_scales[:, c, cols],
-                                start=(c == 0),
-                                stop=(c == PASSES - 1),
-                            )
-                        nc.scalar.copy(out=result[:, i, cols], in_=acc[:])
-                nc.sync.dma_start(out=out_rows[a][:, r0 : r0 + PAIR, :], in_=result[:])
+            if before is not None:
+                unit_before, grouped_before = before
+                codes_before, scales_before = quantise_tokens(unit_before[2], grouped_before)
+            add_halves(n, products, gq_rows)
+            if i == 0:
+                for q in range(HID // P // PAIR):
+                    for c in range(PASSES):
+                        turn(
+                            [w_words[:, PAIR * q + j, :] for j in range(PAIR)], c,
+                            w_grouped[:, c, PAIR * P * q : PAIR * P * (q + 1), :],
+                        )
+            gq_grouped = turn_tokens(n, gq_rows)
+            if before is not None:
+                multiply(unit_before[0], unit_before[1], unit_before[2], codes_before, scales_before)
+            before = ((a, r0, n), gq_grouped)
+        unit_before, grouped_before = before
+        codes_before, scales_before = quantise_tokens(unit_before[2], grouped_before)
+        multiply(unit_before[0], unit_before[1], unit_before[2], codes_before, scales_before)

@@ -175,6 +175,7 @@ def tile_gptossmlaattention_pb_kernel(tc, hidden_states, cos, sin, Wq, bq, grad_
             if before is not None:
                 unit_before, grouped_before = before
                 codes_before, scales_before = quantise_tokens(unit_before[2], grouped_before)
+                multiply(unit_before[0], unit_before[1], unit_before[2], codes_before, scales_before)
             add_halves(n, products, gq_rows)
             if i == 0:
                 for q in range(HID // P // PAIR):
@@ -183,10 +184,7 @@ def tile_gptossmlaattention_pb_kernel(tc, hidden_states, cos, sin, Wq, bq, grad_
                             [w_words[:, PAIR * q + j, :] for j in range(PAIR)], c,
                             w_grouped[:, c, PAIR * P * q : PAIR * P * (q + 1), :],
                         )
-            gq_grouped = turn_tokens(n, gq_rows)
-            if before is not None:
-                multiply(unit_before[0], unit_before[1], unit_before[2], codes_before, scales_before)
-            before = ((a, r0, n), gq_grouped)
+            before = ((a, r0, n), turn_tokens(n, gq_rows))
         unit_before, grouped_before = before
         codes_before, scales_before = quantise_tokens(unit_before[2], grouped_before)
         multiply(unit_before[0], unit_before[1], unit_before[2], codes_before, scales_before)

@@ -39,15 +39,19 @@ def tile_gptossmlaattention_pb_kernel(tc, hidden_states, cos, sin, Wq, bq, grad_
     with ExitStack() as ctx:
         keep = ctx.enter_context(tc.tile_pool(name="keep", bufs=1))
         stage = ctx.enter_context(tc.tile_pool(name="stage", bufs=2))
+        wide = ctx.enter_context(tc.tile_pool(name="wide", bufs=3))
         results = ctx.enter_context(tc.tile_pool(name="results", bufs=3))
-        turned = ctx.enter_context(tc.psum_pool(name="turned", bufs=4))
-        sums = ctx.enter_context(tc.psum_pool(name="sums", bufs=4))
+        turned = ctx.enter_context(tc.psum_pool(name="turned", bufs=3))
+        sums = ctx.enter_context(tc.psum_pool(name="sums", bufs=3))
+        spread = ctx.enter_context(tc.psum_pool(name="spread", bufs=2))
         ctx.enter_context(tc.manual_schedule())
 
         ident = keep.tile([P, P], F32)
         make_identity(nc, ident[:])
+        ident_bf = keep.tile([P, P], BF16)
+        make_identity(nc, ident_bf[:])
 
-        tables = keep.tile([P, 2, CHUNKS, PAIR * ROPE], BF16)
+        tables = keep.tile([P, CHUNKS, 2, PAIR * ROPE], BF16)
         grads = [keep.tile([P, HEADS, PAIR * HEAD], BF16, name="grads%d" % a) for a in range(CHUNKS)]
         w_rows = keep.tile([P, HID // P, K], BF16)
         grad_chunks = grad_out.rearrange("b h (a p r) d -> a p (b h) (r d)", p=P, r=PAIR)
@@ -55,13 +59,13 @@ def tile_gptossmlaattention_pb_kernel(tc, hidden_states, cos, sin, Wq, bq, grad_
         w_view = Wq.rearrange("(j p) k -> p j k", p=P)
         out_rows = out.rearrange("b (a p r) n -> a p (b r) n", p=P, r=PAIR)
         for x in range(2):
-            nc.sync.dma_start(out=tables[:, x, 0:2], in_=table_views[x][:, 0:2])
+            nc.sync.dma_start(out=tables[:, 0:2, x], in_=table_views[x][:, 0:2])
         for a in range(2):
             nc.sync.dma_start(out=grads[a][:], in_=grad_chunks[a])
         for q in range(HID // P // PAIR):
             nc.sync.dma_start(out=w_rows[:, PAIR * q : PAIR * (q + 1), :], in_=w_view[:, PAIR * q : PAIR * (q + 1), :])
         for x in range(2):
-            nc.sync.dma_start(out=tables[:, x, 2:CHUNKS], in_=table_views[x][:, 2:CHUNKS])
+            nc.sync.dma_start(out=tables[:, 2:CHUNKS, x], in_=table_views[x][:, 2:CHUNKS])
         for a in range(2, CHUNKS):
             nc.sync.dma_start(out=grads[a][:], in_=grad_chunks[a])
 
@@ -77,17 +81,25 @@ def tile_gptossmlaattention_pb_kernel(tc, hidden_states, cos, sin, Wq, bq, grad_
                     )
             nc.scalar.copy(out=grouped.bitcast(F32), in_=bank[:].rearrange("p u n -> p n u"))
 
-        def products_of(a, r0, n):
-            products = stage.tile([P, 2, PAIR, HEADS, ROPE], F32)
+        def tables_to_psum(a):
+            bank = spread.tile([P, 2, PAIR, ROPE], F32)
+            nc.tensor.matmul(
+                bank[:].rearrange("p x r d -> p (x r d)"),
+                lhsT=ident_bf[:],
+                rhs=tables[:, a].rearrange("p x n -> p (x n)"),
+                start=True,
+                stop=True,
+            )
+            return bank
+
+        def products_of(a, r0, n, bank):
+            products = wide.tile([P, 2, PAIR, HEADS, ROPE], F32)
             by_token = grads[a][:].rearrange("p h (r d) -> p r h d", r=PAIR)
             for x in range(2):
                 nc.vector.tensor_tensor(
                     out=products[:, x, 0:n],
                     in0=by_token[:, r0 : r0 + n, :, NOPE:HEAD],
-                    in1=tables[:, x, a, r0 * ROPE : (r0 + n) * ROPE]
-                    .rearrange("p (r d) -> p r d", r=n)
-                    .unsqueeze(2)
-                    .to_broadcast([P, n, HEADS, ROPE]),
+                    in1=bank[:, x, r0 : r0 + n, :].unsqueeze(2).to_broadcast([P, n, HEADS, ROPE]),
                     op=ALU.mult,
                 )
             return products
@@ -103,13 +115,13 @@ def tile_gptossmlaattention_pb_kernel(tc, hidden_states, cos, sin, Wq, bq, grad_
 
         def add_halves(n, products, gq_rows):
             gq_heads = gq_rows[:].rearrange("p r (h d) -> p r h d", h=HEADS)
-            nc.vector.tensor_tensor(
+            nc.gpsimd.tensor_tensor(
                 out=gq_heads[:, 0:n, :, NOPE : NOPE + HALF],
                 in0=products[:, 0, 0:n, :, 0:HALF],
                 in1=products[:, 1, 0:n, :, HALF:ROPE],
                 op=ALU.add,
             )
-            nc.vector.tensor_tensor(
+            nc.gpsimd.tensor_tensor(
                 out=gq_heads[:, 0:n, :, NOPE + HALF : HEAD],
                 in0=products[:, 0, 0:n, :, HALF:ROPE],
                 in1=products[:, 1, 0:n, :, 0:HALF],
@@ -155,36 +167,46 @@ def tile_gptossmlaattention_pb_kernel(tc, hidden_states, cos, sin, Wq, bq, grad_
             nc.sync.dma_start(out=out_rows[a][:, r0 : r0 + n, :], in_=result[:, 0:n, :])
 
         units = [(a, 0, PAIR) for a in range(CHUNKS - 1)] + [(CHUNKS - 1, r, 1) for r in range(PAIR)]
+        count = len(units)
 
         w_grouped = keep.tile([P, PASSES, HID, PACK], BF16, align_bytes=64)
         w_codes = keep.tile([P, PASSES, HID], U32, align_bytes=64)
         w_scales = keep.tile([P, PASSES, HID], U8, align_bytes=64)
         w_words = w_rows[:].bitcast(F32)
 
-        before = None
-        for i, (a, r0, n) in enumerate(units):
-            products = products_of(a, r0, n)
-            gq_rows = unrotated_of(a, r0, n)
-            if i == 1:
-                for c in range(PASSES):
-                    nc.vector.quantize_mx(
-                        out=w_codes[:, c, :].bitcast(E4M3X4),
-                        scales=w_scales[:, c, :],
-                        in_=w_grouped[:, c].rearrange("p n t -> p (n t)"),
-                    )
-            if before is not None:
-                unit_before, grouped_before = before
-                codes_before, scales_before = quantise_tokens(unit_before[2], grouped_before)
-                multiply(unit_before[0], unit_before[1], unit_before[2], codes_before, scales_before)
-            add_halves(n, products, gq_rows)
-            if i == 0:
+        banks = {0: tables_to_psum(0)}
+        products = {}
+        rows_of = {}
+        grouped_of = {}
+        codes_of = {}
+        for s in range(count + 3):
+            if s + 1 < count and units[s + 1][0] not in banks:
+                banks[units[s + 1][0]] = tables_to_psum(units[s + 1][0])
+            if s < count:
+                a, r0, n = units[s]
+                products[s] = products_of(a, r0, n, banks[a])
+            if 0 <= s - 1 < count:
+                a, r0, n = units[s - 1]
+                rows_of[s - 1] = unrotated_of(a, r0, n)
+                add_halves(n, products[s - 1], rows_of[s - 1])
+            if s == 0:
                 for q in range(HID // P // PAIR):
                     for c in range(PASSES):
                         turn(
                             [w_words[:, PAIR * q + j, :] for j in range(PAIR)], c,
                             w_grouped[:, c, PAIR * P * q : PAIR * P * (q + 1), :],
                         )
-            before = ((a, r0, n), turn_tokens(n, gq_rows))
-        unit_before, grouped_before = before
-        codes_before, scales_before = quantise_tokens(unit_before[2], grouped_before)
-        multiply(unit_before[0], unit_before[1], unit_before[2], codes_before, scales_before)
+            if 0 <= s - 2 < count:
+                grouped_of[s - 2] = turn_tokens(units[s - 2][2], rows_of[s - 2])
+            if s == 2:
+                for c in range(PASSES):
+                    nc.vector.quantize_mx(
+                        out=w_codes[:, c, :].bitcast(E4M3X4),
+                        scales=w_scales[:, c, :],
+                        in_=w_grouped[:, c].rearrange("p n t -> p (n t)"),
+                    )
+            if 0 <= s - 3 < count:
+                a, r0, n = units[s - 3]
+                multiply(a, r0, n, codes_of[s - 3][0], codes_of[s - 3][1])
+            if 0 <= s - 2 < count:
+                codes_of[s - 2] = quantise_tokens(units[s - 2][2], grouped_of[s - 2])

@@ -50,6 +50,8 @@ def tile_gptossmlaattention_pb_kernel(tc, hidden_states, cos, sin, Wq, bq, grad_
         make_identity(nc, ident[:])
         ident_bf = keep.tile([P, P], BF16)
         make_identity(nc, ident_bf[:])
+        minus_ident_bf = keep.tile([P, P], BF16)
+        nc.scalar.mul(out=minus_ident_bf[:], in_=ident_bf[:], mul=-1.0)
 
         tables = keep.tile([P, CHUNKS, 2, PAIR * ROPE], BF16)
         grads = [keep.tile([P, HEADS, PAIR * HEAD], BF16, name="grads%d" % a) for a in range(CHUNKS)]
@@ -83,29 +85,42 @@ def tile_gptossmlaattention_pb_kernel(tc, hidden_states, cos, sin, Wq, bq, grad_
 
         def tables_to_psum(a):
             bank = spread.tile([P, 2, PAIR, ROPE], F32)
+            by_row = tables[:, a].rearrange("p x (r d) -> p x r d", r=PAIR)
+            nc.tensor.matmul(bank[:, 0], lhsT=ident_bf[:], rhs=by_row[:, 0], start=True, stop=True)
             nc.tensor.matmul(
-                bank[:].rearrange("p x r d -> p (x r d)"),
-                lhsT=ident_bf[:],
-                rhs=tables[:, a].rearrange("p x n -> p (x n)"),
-                start=True,
-                stop=True,
+                bank[:, 1, :, HALF:ROPE], lhsT=ident_bf[:], rhs=by_row[:, 1, :, HALF:ROPE], start=True, stop=True
+            )
+            nc.tensor.matmul(
+                bank[:, 1, :, 0:HALF], lhsT=minus_ident_bf[:], rhs=by_row[:, 1, :, 0:HALF], start=True, stop=True
             )
             return bank
 
         def products_of(a, r0, n, bank):
             products = wide.tile([P, 2, PAIR, HEADS, ROPE], F32)
-            by_token = grads[a][:].rearrange("p h (r d) -> p r h d", r=PAIR)
-            for x in range(2):
-                nc.vector.tensor_tensor(
-                    out=products[:, x, 0:n],
-                    in0=by_token[:, r0 : r0 + n, :, NOPE:HEAD],
-                    in1=bank[:, x, r0 : r0 + n, :].unsqueeze(2).to_broadcast([P, n, HEADS, ROPE]),
-                    op=ALU.mult,
-                )
+            by_token = grads[a][:].rearrange("p h (r d) -> p r h d", r=PAIR)[:, r0 : r0 + n]
+
+            def table(x, d0, d1):
+                return bank[:, x, r0 : r0 + n, d0:d1].unsqueeze(2).to_broadcast([P, n, HEADS, d1 - d0])
+
+            nc.vector.tensor_tensor(
+                out=products[:, 0, 0:n], in0=by_token[:, :, :, NOPE:HEAD], in1=table(0, 0, ROPE), op=ALU.mult
+            )
+            nc.vector.tensor_tensor(
+                out=products[:, 1, 0:n, :, 0:HALF],
+                in0=by_token[:, :, :, NOPE + HALF : HEAD],
+                in1=table(1, HALF, ROPE),
+                op=ALU.mult,
+            )
+            nc.vector.tensor_tensor(
+                out=products[:, 1, 0:n, :, HALF:ROPE],
+                in0=by_token[:, :, :, NOPE : NOPE + HALF],
+                in1=table(1, 0, HALF),
+                op=ALU.mult,
+            )
             return products
 
         def unrotated_of(a, r0, n):
-            gq_rows = stage.tile([P, PAIR, K], BF16)
+            gq_rows = wide.tile([P, PAIR, K], BF16)
             by_token_words = grads[a][:].bitcast(F32).rearrange("p h (r w) -> p r h w", r=PAIR)
             nc.scalar.copy(
                 out=gq_rows[:].bitcast(F32).rearrange("p r (h w) -> p r h w", h=HEADS)[:, 0:n, :, 0 : NOPE // 2],
@@ -113,19 +128,10 @@ def tile_gptossmlaattention_pb_kernel(tc, hidden_states, cos, sin, Wq, bq, grad_
             )
             return gq_rows
 
-        def add_halves(n, products, gq_rows):
+        def add_terms(engine, n, products, gq_rows):
             gq_heads = gq_rows[:].rearrange("p r (h d) -> p r h d", h=HEADS)
-            nc.gpsimd.tensor_tensor(
-                out=gq_heads[:, 0:n, :, NOPE : NOPE + HALF],
-                in0=products[:, 0, 0:n, :, 0:HALF],
-                in1=products[:, 1, 0:n, :, HALF:ROPE],
-                op=ALU.add,
-            )
-            nc.gpsimd.tensor_tensor(
-                out=gq_heads[:, 0:n, :, NOPE + HALF : HEAD],
-                in0=products[:, 0, 0:n, :, HALF:ROPE],
-                in1=products[:, 1, 0:n, :, 0:HALF],
-                op=ALU.subtract,
+            engine.tensor_tensor(
+                out=gq_heads[:, 0:n, :, NOPE:HEAD], in0=products[:, 0, 0:n], in1=products[:, 1, 0:n], op=ALU.add
             )
 
         def turn_tokens(n, gq_rows):
@@ -166,14 +172,25 @@ def tile_gptossmlaattention_pb_kernel(tc, hidden_states, cos, sin, Wq, bq, grad_
                     nc.scalar.copy(out=result[:, i, cols], in_=acc[:])
             nc.sync.dma_start(out=out_rows[a][:, r0 : r0 + n, :], in_=result[:, 0:n, :])
 
-        units = [(a, 0, PAIR) for a in range(CHUNKS - 1)] + [(CHUNKS - 1, r, 1) for r in range(PAIR)]
+        units = [(a, 0, PAIR) for a in range(CHUNKS - 2)] + [(a, r, 1) for a in (CHUNKS - 2, CHUNKS - 1) for r in range(PAIR)]
         count = len(units)
+        adders = [nc.gpsimd] * (count - 2) + [nc.vector] * 2
 
         w_grouped = keep.tile([P, PASSES, HID, PACK], BF16, align_bytes=64)
         w_codes = keep.tile([P, PASSES, HID], U32, align_bytes=64)
         w_scales = keep.tile([P, PASSES, HID], U8, align_bytes=64)
         w_words = w_rows[:].bitcast(F32)
 
+        def quantise_w(q):
+            cols = slice(PAIR * P * q, PAIR * P * (q + 1))
+            for c in range(PASSES):
+                nc.vector.quantize_mx(
+                    out=w_codes[:, c, cols].bitcast(E4M3X4),
+                    scales=w_scales[:, c, cols],
+                    in_=w_grouped[:, c, cols, :].rearrange("p n t -> p (n t)"),
+                )
+
+        quantise_w_after = {0: [0], 1: [1, 2, 3]}
         banks = {0: tables_to_psum(0)}
         products = {}
         rows_of = {}
@@ -184,11 +201,8 @@ def tile_gptossmlaattention_pb_kernel(tc, hidden_states, cos, sin, Wq, bq, grad_
                 banks[units[s + 1][0]] = tables_to_psum(units[s + 1][0])
             if s < count:
                 a, r0, n = units[s]
+                rows_of[s] = unrotated_of(a, r0, n)
                 products[s] = products_of(a, r0, n, banks[a])
-            if 0 <= s - 1 < count:
-                a, r0, n = units[s - 1]
-                rows_of[s - 1] = unrotated_of(a, r0, n)
-                add_halves(n, products[s - 1], rows_of[s - 1])
             if s == 0:
                 for q in range(HID // P // PAIR):
                     for c in range(PASSES):
@@ -196,15 +210,12 @@ def tile_gptossmlaattention_pb_kernel(tc, hidden_states, cos, sin, Wq, bq, grad_
                             [w_words[:, PAIR * q + j, :] for j in range(PAIR)], c,
                             w_grouped[:, c, PAIR * P * q : PAIR * P * (q + 1), :],
                         )
+            for q in quantise_w_after.get(s, []):
+                quantise_w(q)
+            if 0 <= s - 1 < count:
+                add_terms(adders[s - 1], units[s - 1][2], products[s - 1], rows_of[s - 1])
             if 0 <= s - 2 < count:
                 grouped_of[s - 2] = turn_tokens(units[s - 2][2], rows_of[s - 2])
-            if s == 2:
-                for c in range(PASSES):
-                    nc.vector.quantize_mx(
-                        out=w_codes[:, c, :].bitcast(E4M3X4),
-                        scales=w_scales[:, c, :],
-                        in_=w_grouped[:, c].rearrange("p n t -> p (n t)"),
-                    )
             if 0 <= s - 3 < count:
                 a, r0, n = units[s - 3]
                 multiply(a, r0, n, codes_of[s - 3][0], codes_of[s - 3][1])

@@ -190,7 +190,9 @@ def tile_gptossmlaattention_pb_kernel(tc, hidden_states, cos, sin, Wq, bq, grad_
                     in_=w_grouped[:, c, cols, :].rearrange("p n t -> p (n t)"),
                 )
 
-        quantise_w_after = {0: [0], 1: [1, 2, 3]}
+        def early(u):
+            return 1 if u == 0 else 0
+
         banks = {0: tables_to_psum(0)}
         products = {}
         rows_of = {}
@@ -210,14 +212,18 @@ def tile_gptossmlaattention_pb_kernel(tc, hidden_states, cos, sin, Wq, bq, grad_
                             [w_words[:, PAIR * q + j, :] for j in range(PAIR)], c,
                             w_grouped[:, c, PAIR * P * q : PAIR * P * (q + 1), :],
                         )
-            for q in quantise_w_after.get(s, []):
-                quantise_w(q)
+            if s == 1:
+                for q in range(HID // P // PAIR):
+                    quantise_w(q)
             if 0 <= s - 1 < count:
                 add_terms(adders[s - 1], units[s - 1][2], products[s - 1], rows_of[s - 1])
-            if 0 <= s - 2 < count:
-                grouped_of[s - 2] = turn_tokens(units[s - 2][2], rows_of[s - 2])
-            if 0 <= s - 3 < count:
-                a, r0, n = units[s - 3]
-                multiply(a, r0, n, codes_of[s - 3][0], codes_of[s - 3][1])
-            if 0 <= s - 2 < count:
-                codes_of[s - 2] = quantise_tokens(units[s - 2][2], grouped_of[s - 2])
+            for u in range(count):
+                if u + 2 - early(u) == s:
+                    grouped_of[u] = turn_tokens(units[u][2], rows_of[u])
+            for u in range(count):
+                if u + 3 - early(u) == s:
+                    a, r0, n = units[u]
+                    multiply(a, r0, n, codes_of[u][0], codes_of[u][1])
+            for u in range(count):
+                if u + 2 - early(u) == s:
+                    codes_of[u] = quantise_tokens(units[u][2], grouped_of[u])

@@ -193,6 +193,9 @@ def tile_gptossmlaattention_pb_kernel(tc, hidden_states, cos, sin, Wq, bq, grad_
         def early(u):
             return 1 if u == 0 else 0
 
+        def hold_gpsimd(read_by_quantise):
+            nc.gpsimd.memset(read_by_quantise, 0.0)
+
         banks = {0: tables_to_psum(0)}
         products = {}
         rows_of = {}
@@ -212,11 +215,12 @@ def tile_gptossmlaattention_pb_kernel(tc, hidden_states, cos, sin, Wq, bq, grad_
                             [w_words[:, PAIR * q + j, :] for j in range(PAIR)], c,
                             w_grouped[:, c, PAIR * P * q : PAIR * P * (q + 1), :],
                         )
+            if 0 <= s - 1 < count:
+                add_terms(adders[s - 1], units[s - 1][2], products[s - 1], rows_of[s - 1])
             if s == 1:
                 for q in range(HID // P // PAIR):
                     quantise_w(q)
-            if 0 <= s - 1 < count:
-                add_terms(adders[s - 1], units[s - 1][2], products[s - 1], rows_of[s - 1])
+                hold_gpsimd(w_grouped[:, PASSES - 1, HID - 1, 0:2])
             for u in range(count):
                 if u + 2 - early(u) == s:
                     grouped_of[u] = turn_tokens(units[u][2], rows_of[u])
@@ -227,3 +231,4 @@ def tile_gptossmlaattention_pb_kernel(tc, hidden_states, cos, sin, Wq, bq, grad_
             for u in range(count):
                 if u + 2 - early(u) == s:
                     codes_of[u] = quantise_tokens(units[u][2], grouped_of[u])
+                    hold_gpsimd(grouped_of[u][:, PASSES - 1, 0, 0:2])

@@ -83,62 +83,77 @@ def tile_gptossmlaattention_pb_kernel(tc, hidden_states, cos, sin, Wq, bq, grad_
                     )
             nc.scalar.copy(out=grouped.bitcast(F32), in_=bank[:].rearrange("p u n -> p n u"))
 
+        Q_NOPE = NOPE // PACK
+        Q_HALF = HALF // PACK
+
         def tables_to_psum(a):
-            bank = spread.tile([P, 2, PAIR, ROPE], F32)
-            by_row = tables[:, a].rearrange("p x (r d) -> p x r d", r=PAIR)
-            nc.tensor.matmul(bank[:, 0], lhsT=ident_bf[:], rhs=by_row[:, 0], start=True, stop=True)
-            nc.tensor.matmul(
-                bank[:, 1, :, HALF:ROPE], lhsT=ident_bf[:], rhs=by_row[:, 1, :, HALF:ROPE], start=True, stop=True
-            )
-            nc.tensor.matmul(
-                bank[:, 1, :, 0:HALF], lhsT=minus_ident_bf[:], rhs=by_row[:, 1, :, 0:HALF], start=True, stop=True
-            )
+            bank = spread.tile([P, 2, 2, PAIR, HALF], F32)
+            quads = tables[:, a].rearrange("p x (r q f e) -> p x r q f e", r=PAIR, f=2, e=2)
+            places = bank[:].rearrange("p x f r (q e) -> p x f r q e", e=2)
+            for f in range(2):
+                nc.tensor.matmul(places[:, 0, f], lhsT=ident_bf[:], rhs=quads[:, 0, :, :, f, :], start=True, stop=True)
+                nc.tensor.matmul(
+                    places[:, 1, f, :, Q_HALF:], lhsT=ident_bf[:], rhs=quads[:, 1, :, Q_HALF:, f, :], start=True, stop=True
+                )
+                nc.tensor.matmul(
+                    places[:, 1, f, :, 0:Q_HALF], lhsT=minus_ident_bf[:], rhs=quads[:, 1, :, 0:Q_HALF, f, :],
+                    start=True, stop=True,
+                )
             return bank
 
         def products_of(a, r0, n, bank):
-            products = wide.tile([P, 2, PAIR, HEADS, ROPE], F32)
-            by_token = grads[a][:].rearrange("p h (r d) -> p r h d", r=PAIR)[:, r0 : r0 + n]
+            products = wide.tile([P, 2, HEADS, 2, PAIR, HALF], F32)
+            quads = grads[a][:].rearrange("p h (r q f e) -> p h r q f e", r=PAIR, f=2, e=2)[:, :, r0 : r0 + n]
+            places = products[:].rearrange("p x h f r (q e) -> p x h f r q e", e=2)[:, :, :, :, 0:n]
+            tabled = bank[:].rearrange("p x f r (q e) -> p x f r q e", e=2)[:, :, :, r0 : r0 + n]
 
-            def table(x, d0, d1):
-                return bank[:, x, r0 : r0 + n, d0:d1].unsqueeze(2).to_broadcast([P, n, HEADS, d1 - d0])
+            def multiply_quads(f, x, out_q, in_q, table_q):
+                count_q = out_q[1]
+                nc.vector.tensor_tensor(
+                    out=places[:, x, :, f, :, out_q[0] : out_q[0] + count_q],
+                    in0=quads[:, :, :, Q_NOPE + in_q : Q_NOPE + in_q + count_q, f, :],
+                    in1=tabled[:, x, f, :, table_q : table_q + count_q]
+                    .unsqueeze(1)
+                    .to_broadcast([P, HEADS, n, count_q, 2]),
+                    op=ALU.mult,
+                )
 
-            nc.vector.tensor_tensor(
-                out=products[:, 0, 0:n], in0=by_token[:, :, :, NOPE:HEAD], in1=table(0, 0, ROPE), op=ALU.mult
-            )
-            nc.vector.tensor_tensor(
-                out=products[:, 1, 0:n, :, 0:HALF],
-                in0=by_token[:, :, :, NOPE + HALF : HEAD],
-                in1=table(1, HALF, ROPE),
-                op=ALU.mult,
-            )
-            nc.vector.tensor_tensor(
-                out=products[:, 1, 0:n, :, HALF:ROPE],
-                in0=by_token[:, :, :, NOPE : NOPE + HALF],
-                in1=table(1, 0, HALF),
-                op=ALU.mult,
-            )
+            for f in range(2):
+                multiply_quads(f, 0, (0, 2 * Q_HALF), 0, 0)
+                multiply_quads(f, 1, (0, Q_HALF), Q_HALF, Q_HALF)
+                multiply_quads(f, 1, (Q_HALF, Q_HALF), 0, 0)
             return products
 
         def unrotated_of(a, r0, n):
-            gq_rows = wide.tile([P, PAIR, K], BF16)
-            by_token_words = grads[a][:].bitcast(F32).rearrange("p h (r w) -> p r h w", r=PAIR)
-            nc.scalar.copy(
-                out=gq_rows[:].bitcast(F32).rearrange("p r (h w) -> p r h w", h=HEADS)[:, 0:n, :, 0 : NOPE // 2],
-                in_=by_token_words[:, r0 : r0 + n, :, 0 : NOPE // 2],
-            )
+            gq_rows = wide.tile([P, 2, PAIR, K // 2], BF16)
+            words = grads[a][:].bitcast(F32).rearrange("p h (r q f) -> p h r q f", r=PAIR, f=2)
+            places = gq_rows[:].bitcast(F32).rearrange("p f r (h q) -> p f h r q", h=HEADS)
+            for f in range(2):
+                nc.scalar.copy(out=places[:, f, :, 0:n, 0:Q_NOPE], in_=words[:, :, r0 : r0 + n, 0:Q_NOPE, f])
             return gq_rows
 
         def add_terms(engine, n, products, gq_rows):
-            gq_heads = gq_rows[:].rearrange("p r (h d) -> p r h d", h=HEADS)
+            places = gq_rows[:].rearrange("p f r (h j) -> p h f r j", h=HEADS)
             engine.tensor_tensor(
-                out=gq_heads[:, 0:n, :, NOPE:HEAD], in0=products[:, 0, 0:n], in1=products[:, 1, 0:n], op=ALU.add
+                out=places[:, :, :, 0:n, 2 * Q_NOPE :],
+                in0=products[:, 0, :, :, 0:n],
+                in1=products[:, 1, :, :, 0:n],
+                op=ALU.add,
             )
 
         def turn_tokens(n, gq_rows):
             gq_grouped = stage.tile([P, PASSES, PAIR * P, PACK], BF16, align_bytes=64)
             gq_words = gq_rows[:].bitcast(F32)
             for c in range(PASSES):
-                turn([gq_words[:, i, :] for i in range(n)], c, gq_grouped[:, c, 0 : n * P, :])
+                bank = turned.tile([P, 2, n * P], F32, tag="turned")
+                for i in range(n):
+                    for f in range(2):
+                        nc.tensor.transpose(
+                            bank[:, f, i * P : (i + 1) * P], gq_words[:, f, i, P * c : P * (c + 1)], ident[:]
+                        )
+                nc.scalar.copy(
+                    out=gq_grouped[:, c, 0 : n * P, :].bitcast(F32), in_=bank[:].rearrange("p f n -> p n f")
+                )
             return gq_grouped
 
         def quantise_tokens(n, gq_grouped):
@@ -152,7 +167,7 @@ def tile_gptossmlaattention_pb_kernel(tc, hidden_states, cos, sin, Wq, bq, grad_
                 )
             return gq_codes, gq_scales
 
-        def multiply(a, r0, n, gq_codes, gq_scales):
+        def multiply(a, r0, n, gq_codes, gq_scales, last):
             result = results.tile([P, PAIR, HID], F32)
             for i in range(n):
                 rows = slice(i * P, (i + 1) * P)
@@ -170,19 +185,22 @@ def tile_gptossmlaattention_pb_kernel(tc, hidden_states, cos, sin, Wq, bq, grad_
                             stop=(c == PASSES - 1),
                         )
                     nc.scalar.copy(out=result[:, i, cols], in_=acc[:])
-            nc.sync.dma_start(out=out_rows[a][:, r0 : r0 + n, :], in_=result[:, 0:n, :])
+                    if last:
+                        nc.sync.dma_start(out=out_rows[a][:, r0 + i, cols], in_=result[:, i, cols])
+            if not last:
+                nc.sync.dma_start(out=out_rows[a][:, r0 : r0 + n, :], in_=result[:, 0:n, :])
 
         units = [(a, 0, PAIR) for a in range(CHUNKS - 2)] + [(a, r, 1) for a in (CHUNKS - 2, CHUNKS - 1) for r in range(PAIR)]
         count = len(units)
-        adders = [nc.gpsimd] * (count - 2) + [nc.vector] * 2
+        adders = [nc.gpsimd] * (count - 1) + [nc.vector]
 
         w_grouped = keep.tile([P, PASSES, HID, PACK], BF16, align_bytes=64)
         w_codes = keep.tile([P, PASSES, HID], U32, align_bytes=64)
         w_scales = keep.tile([P, PASSES, HID], U8, align_bytes=64)
         w_words = w_rows[:].bitcast(F32)
 
-        def quantise_w(q):
-            cols = slice(PAIR * P * q, PAIR * P * (q + 1))
+        def quantise_w(half):
+            cols = slice(N_TILE * half, N_TILE * (half + 1))
             for c in range(PASSES):
                 nc.vector.quantize_mx(
                     out=w_codes[:, c, cols].bitcast(E4M3X4),
@@ -204,9 +222,11 @@ def tile_gptossmlaattention_pb_kernel(tc, hidden_states, cos, sin, Wq, bq, grad_
         for s in range(count + 3):
             if s + 1 < count and units[s + 1][0] not in banks:
                 banks[units[s + 1][0]] = tables_to_psum(units[s + 1][0])
+            for u in {0: [0, 1], 1: []}.get(s, [s]):
+                if u < count:
+                    rows_of[u] = unrotated_of(units[u][0], units[u][1], units[u][2])
             if s < count:
                 a, r0, n = units[s]
-                rows_of[s] = unrotated_of(a, r0, n)
                 products[s] = products_of(a, r0, n, banks[a])
             if s == 0:
                 for q in range(HID // P // PAIR):
@@ -218,8 +238,8 @@ def tile_gptossmlaattention_pb_kernel(tc, hidden_states, cos, sin, Wq, bq, grad_
             if 0 <= s - 1 < count:
                 add_terms(adders[s - 1], units[s - 1][2], products[s - 1], rows_of[s - 1])
             if s == 1:
-                for q in range(HID // P // PAIR):
-                    quantise_w(q)
+                for half in range(N_HALVES):
+                    quantise_w(half)
                 hold_gpsimd(w_grouped[:, PASSES - 1, HID - 1, 0:2])
             for u in range(count):
                 if u + 2 - early(u) == s:
@@ -227,7 +247,7 @@ def tile_gptossmlaattention_pb_kernel(tc, hidden_states, cos, sin, Wq, bq, grad_
             for u in range(count):
                 if u + 3 - early(u) == s:
                     a, r0, n = units[u]
-                    multiply(a, r0, n, codes_of[u][0], codes_of[u][1])
+                    multiply(a, r0, n, codes_of[u][0], codes_of[u][1], u == count - 1)
             for u in range(count):
                 if u + 2 - early(u) == s:
                     codes_of[u] = quantise_tokens(units[u][2], grouped_of[u])

@@ -54,7 +54,8 @@ def tile_gptossmlaattention_pb_kernel(tc, hidden_states, cos, sin, Wq, bq, grad_
         nc.scalar.mul(out=minus_ident_bf[:], in_=ident_bf[:], mul=-1.0)
 
         tables = keep.tile([P, CHUNKS, 2, PAIR * ROPE], BF16)
-        grads = [keep.tile([P, HEADS, PAIR * HEAD], BF16, name="grads%d" % a) for a in range(CHUNKS)]
+        first_grads = [keep.tile([P, HEADS, HEAD], BF16, name="first_grads%d" % r) for r in range(PAIR)]
+        grads = [None] + [keep.tile([P, HEADS, PAIR * HEAD], BF16, name="grads%d" % a) for a in range(1, CHUNKS)]
         w_rows = keep.tile([P, HID // P, K], BF16)
         grad_chunks = grad_out.rearrange("b h (a p r) d -> a p (b h) (r d)", p=P, r=PAIR)
         table_views = [x.rearrange("b (a p r) d -> p (b a) (r d)", p=P, r=PAIR) for x in (cos, sin)]
@@ -62,14 +63,27 @@ def tile_gptossmlaattention_pb_kernel(tc, hidden_states, cos, sin, Wq, bq, grad_
         out_rows = out.rearrange("b (a p r) n -> a p (b r) n", p=P, r=PAIR)
         for x in range(2):
             nc.sync.dma_start(out=tables[:, 0:2, x], in_=table_views[x][:, 0:2])
-        for a in range(2):
-            nc.sync.dma_start(out=grads[a][:], in_=grad_chunks[a])
-        for q in range(HID // P // PAIR):
+        def load_w(q):
             nc.sync.dma_start(out=w_rows[:, PAIR * q : PAIR * (q + 1), :], in_=w_view[:, PAIR * q : PAIR * (q + 1), :])
+
+        for r in range(PAIR):
+            nc.sync.dma_start(out=first_grads[r][:], in_=grad_chunks[0][:, :, r * HEAD : (r + 1) * HEAD])
+        nc.sync.dma_start(out=grads[1][:], in_=grad_chunks[1])
+        load_w(0)
+        load_w(1)
         for x in range(2):
             nc.sync.dma_start(out=tables[:, 2:CHUNKS, x], in_=table_views[x][:, 2:CHUNKS])
-        for a in range(2, CHUNKS):
+        nc.sync.dma_start(out=grads[2][:], in_=grad_chunks[2])
+        load_w(2)
+        load_w(3)
+        for a in range(3, CHUNKS):
             nc.sync.dma_start(out=grads[a][:], in_=grad_chunks[a])
+
+        def rows_of_chunk(a, r0, n):
+            if a == 0:
+                assert n == 1
+                return first_grads[r0][:]
+            return grads[a][:, :, r0 * HEAD : (r0 + n) * HEAD]
 
         def turn(row_words, c, grouped):
             n = len(row_words)
@@ -103,7 +117,7 @@ def tile_gptossmlaattention_pb_kernel(tc, hidden_states, cos, sin, Wq, bq, grad_
 
         def products_of(a, r0, n, bank):
             products = wide.tile([P, 2, HEADS, 2, PAIR, HALF], F32)
-            quads = grads[a][:].rearrange("p h (r q f e) -> p h r q f e", r=PAIR, f=2, e=2)[:, :, r0 : r0 + n]
+            quads = rows_of_chunk(a, r0, n).rearrange("p h (r q f e) -> p h r q f e", r=n, f=2, e=2)
             places = products[:].rearrange("p x h f r (q e) -> p x h f r q e", e=2)[:, :, :, :, 0:n]
             tabled = bank[:].rearrange("p x f r (q e) -> p x f r q e", e=2)[:, :, :, r0 : r0 + n]
 
@@ -126,10 +140,10 @@ def tile_gptossmlaattention_pb_kernel(tc, hidden_states, cos, sin, Wq, bq, grad_
 
         def unrotated_of(a, r0, n):
             gq_rows = wide.tile([P, 2, PAIR, K // 2], BF16)
-            words = grads[a][:].bitcast(F32).rearrange("p h (r q f) -> p h r q f", r=PAIR, f=2)
+            words = rows_of_chunk(a, r0, n).bitcast(F32).rearrange("p h (r q f) -> p h r q f", r=n, f=2)
             places = gq_rows[:].bitcast(F32).rearrange("p f r (h q) -> p f h r q", h=HEADS)
             for f in range(2):
-                nc.scalar.copy(out=places[:, f, :, 0:n, 0:Q_NOPE], in_=words[:, :, r0 : r0 + n, 0:Q_NOPE, f])
+                nc.scalar.copy(out=places[:, f, :, 0:n, 0:Q_NOPE], in_=words[:, :, :, 0:Q_NOPE, f])
             return gq_rows
 
         def add_terms(engine, n, products, gq_rows):
@@ -190,7 +204,10 @@ def tile_gptossmlaattention_pb_kernel(tc, hidden_states, cos, sin, Wq, bq, grad_
             if not last:
                 nc.sync.dma_start(out=out_rows[a][:, r0 : r0 + n, :], in_=result[:, 0:n, :])
 
-        units = [(a, 0, PAIR) for a in range(CHUNKS - 2)] + [(a, r, 1) for a in (CHUNKS - 2, CHUNKS - 1) for r in range(PAIR)]
+        singles = (0, CHUNKS - 2, CHUNKS - 1)
+        units = []
+        for a in range(CHUNKS):
+            units.extend([(a, r, 1) for r in range(PAIR)] if a in singles else [(a, 0, PAIR)])
         count = len(units)
         adders = [nc.gpsimd] * (count - 1) + [nc.vector]
 
@@ -208,13 +225,17 @@ def tile_gptossmlaattention_pb_kernel(tc, hidden_states, cos, sin, Wq, bq, grad_
                     in_=w_grouped[:, c, cols, :].rearrange("p n t -> p (n t)"),
                 )
 
-        def early(u):
-            return 1 if u == 0 else 0
+        def turn_w(q):
+            for c in range(PASSES):
+                turn(
+                    [w_words[:, PAIR * q + j, :] for j in range(PAIR)], c,
+                    w_grouped[:, c, PAIR * P * q : PAIR * P * (q + 1), :],
+                )
 
         def hold_gpsimd(read_by_quantise):
             nc.gpsimd.memset(read_by_quantise, 0.0)
 
-        banks = {0: tables_to_psum(0)}
+        banks = {a: tables_to_psum(a) for a in range(2)}
         products = {}
         rows_of = {}
         grouped_of = {}
@@ -222,33 +243,28 @@ def tile_gptossmlaattention_pb_kernel(tc, hidden_states, cos, sin, Wq, bq, grad_
         for s in range(count + 3):
             if s + 1 < count and units[s + 1][0] not in banks:
                 banks[units[s + 1][0]] = tables_to_psum(units[s + 1][0])
-            for u in {0: [0, 1], 1: []}.get(s, [s]):
+            for u in {0: [0, 1, 2], 1: [], 2: []}.get(s, [s]):
                 if u < count:
                     rows_of[u] = unrotated_of(units[u][0], units[u][1], units[u][2])
             if s < count:
                 a, r0, n = units[s]
                 products[s] = products_of(a, r0, n, banks[a])
             if s == 0:
-                for q in range(HID // P // PAIR):
-                    for c in range(PASSES):
-                        turn(
-                            [w_words[:, PAIR * q + j, :] for j in range(PAIR)], c,
-                            w_grouped[:, c, PAIR * P * q : PAIR * P * (q + 1), :],
-                        )
+                turn_w(0)
+                turn_w(1)
             if 0 <= s - 1 < count:
                 add_terms(adders[s - 1], units[s - 1][2], products[s - 1], rows_of[s - 1])
-            if s == 1:
-                for half in range(N_HALVES):
-                    quantise_w(half)
-                hold_gpsimd(w_grouped[:, PASSES - 1, HID - 1, 0:2])
-            for u in range(count):
-                if u + 2 - early(u) == s:
-                    grouped_of[u] = turn_tokens(units[u][2], rows_of[u])
-            for u in range(count):
-                if u + 3 - early(u) == s:
-                    a, r0, n = units[u]
-                    multiply(a, r0, n, codes_of[u][0], codes_of[u][1], u == count - 1)
-            for u in range(count):
-                if u + 2 - early(u) == s:
-                    codes_of[u] = quantise_tokens(units[u][2], grouped_of[u])
-                    hold_gpsimd(grouped_of[u][:, PASSES - 1, 0, 0:2])
+            if s == 2:
+                quantise_w(0)
+            if 0 <= s - 2 < count:
+                grouped_of[s - 2] = turn_tokens(units[s - 2][2], rows_of[s - 2])
+            if s == 3:
+                turn_w(2)
+                turn_w(3)
+                quantise_w(1)
+            if 0 <= s - 3 < count:
+                a, r0, n = units[s - 3]
+                multiply(a, r0, n, codes_of[s - 3][0], codes_of[s - 3][1], s - 3 == count - 1)
+            if 0 <= s - 2 < count:
+                codes_of[s - 2] = quantise_tokens(units[s - 2][2], grouped_of[s - 2])
+                hold_gpsimd(grouped_of[s - 2][:, PASSES - 2, 0, 0:2])

@@ -26,9 +26,11 @@ PASSES = K // K_PASS
 N_TILE = 512
 N_HALVES = HID // N_TILE
 PAIR = 2
-CHUNK = P * PAIR
-CHUNKS = TOKENS // CHUNK
+CHUNKS = TOKENS // (P * PAIR)
 WORDS = K_PASS // 2
+Q_NOPE = NOPE // PACK
+Q_HALF = HALF // PACK
+PARTS = 2
 
 FLOPS = 2 * TOKENS * HID * K
 BYTES = 2 * (TOKENS * K + HID * K + 2 * TOKENS * ROPE) + 4 * TOKENS * HID
@@ -39,6 +41,7 @@ def tile_gptossmlaattention_pb_kernel(tc, hidden_states, cos, sin, Wq, bq, grad_
     with ExitStack() as ctx:
         keep = ctx.enter_context(tc.tile_pool(name="keep", bufs=1))
         stage = ctx.enter_context(tc.tile_pool(name="stage", bufs=2))
+        coded = ctx.enter_context(tc.tile_pool(name="coded", bufs=3))
         wide = ctx.enter_context(tc.tile_pool(name="wide", bufs=3))
         results = ctx.enter_context(tc.tile_pool(name="results", bufs=3))
         turned = ctx.enter_context(tc.psum_pool(name="turned", bufs=3))
@@ -46,44 +49,44 @@ def tile_gptossmlaattention_pb_kernel(tc, hidden_states, cos, sin, Wq, bq, grad_
         spread = ctx.enter_context(tc.psum_pool(name="spread", bufs=2))
         ctx.enter_context(tc.manual_schedule())
 
-        ident = keep.tile([P, P], F32)
-        make_identity(nc, ident[:])
         ident_bf = keep.tile([P, P], BF16)
         make_identity(nc, ident_bf[:])
         minus_ident_bf = keep.tile([P, P], BF16)
         nc.scalar.mul(out=minus_ident_bf[:], in_=ident_bf[:], mul=-1.0)
+        ident = keep.tile([P, P], F32)
+        make_identity(nc, ident[:])
 
         tables = keep.tile([P, CHUNKS, 2, PAIR * ROPE], BF16)
-        first_grads = [keep.tile([P, HEADS, HEAD], BF16, name="first_grads%d" % r) for r in range(PAIR)]
-        grads = [None] + [keep.tile([P, HEADS, PAIR * HEAD], BF16, name="grads%d" % a) for a in range(1, CHUNKS)]
+        grads = [keep.tile([P, HEADS, PAIR * HEAD], BF16, name="grads%d" % a) for a in range(CHUNKS)]
         w_rows = keep.tile([P, HID // P, K], BF16)
-        grad_chunks = grad_out.rearrange("b h (a p r) d -> a p (b h) (r d)", p=P, r=PAIR)
-        table_views = [x.rearrange("b (a p r) d -> p (b a) (r d)", p=P, r=PAIR) for x in (cos, sin)]
+        grad_chunks = grad_out.rearrange("b h (p a r) d -> a p (b h) (r d)", p=P, r=PAIR)
+        table_views = [x.rearrange("b (p a r) d -> p (b a) (r d)", p=P, r=PAIR) for x in (cos, sin)]
         w_view = Wq.rearrange("(j p) k -> p j k", p=P)
-        out_rows = out.rearrange("b (a p r) n -> a p (b r) n", p=P, r=PAIR)
-        for x in range(2):
-            nc.sync.dma_start(out=tables[:, 0:2, x], in_=table_views[x][:, 0:2])
+        out_rows = out.rearrange("b (p a r) n -> a p (b r) n", p=P, r=PAIR)
+
+        def load_tables(a0, a1):
+            for x in range(2):
+                nc.sync.dma_start(out=tables[:, a0:a1, x], in_=table_views[x][:, a0:a1])
+
+        def load_grads(a, h0=0, h1=HEADS):
+            nc.sync.dma_start(out=grads[a][:, h0:h1], in_=grad_chunks[a][:, h0:h1])
+
         def load_w(q):
             nc.sync.dma_start(out=w_rows[:, PAIR * q : PAIR * (q + 1), :], in_=w_view[:, PAIR * q : PAIR * (q + 1), :])
 
-        for r in range(PAIR):
-            nc.sync.dma_start(out=first_grads[r][:], in_=grad_chunks[0][:, :, r * HEAD : (r + 1) * HEAD])
-        nc.sync.dma_start(out=grads[1][:], in_=grad_chunks[1])
+        load_tables(0, 2)
+        load_grads(0, 0, HEADS // 2)
+        load_grads(0, HEADS // 2, HEADS)
+        load_grads(1)
         load_w(0)
         load_w(1)
-        for x in range(2):
-            nc.sync.dma_start(out=tables[:, 2:CHUNKS, x], in_=table_views[x][:, 2:CHUNKS])
-        nc.sync.dma_start(out=grads[2][:], in_=grad_chunks[2])
+        load_tables(2, 4)
+        load_grads(2)
         load_w(2)
         load_w(3)
+        load_tables(4, CHUNKS)
         for a in range(3, CHUNKS):
-            nc.sync.dma_start(out=grads[a][:], in_=grad_chunks[a])
-
-        def rows_of_chunk(a, r0, n):
-            if a == 0:
-                assert n == 1
-                return first_grads[r0][:]
-            return grads[a][:, :, r0 * HEAD : (r0 + n) * HEAD]
+            load_grads(a)
 
         def turn(row_words, c, grouped):
             n = len(row_words)
@@ -97,14 +100,12 @@ def tile_gptossmlaattention_pb_kernel(tc, hidden_states, cos, sin, Wq, bq, grad_
                     )
             nc.scalar.copy(out=grouped.bitcast(F32), in_=bank[:].rearrange("p u n -> p n u"))
 
-        Q_NOPE = NOPE // PACK
-        Q_HALF = HALF // PACK
 
         def tables_to_psum(a):
-            bank = spread.tile([P, 2, 2, PAIR, HALF], F32)
+            bank = spread.tile([P, 2, PARTS, PAIR, HALF], F32)
             quads = tables[:, a].rearrange("p x (r q f e) -> p x r q f e", r=PAIR, f=2, e=2)
             places = bank[:].rearrange("p x f r (q e) -> p x f r q e", e=2)
-            for f in range(2):
+            for f in range(PARTS):
                 nc.tensor.matmul(places[:, 0, f], lhsT=ident_bf[:], rhs=quads[:, 0, :, :, f, :], start=True, stop=True)
                 nc.tensor.matmul(
                     places[:, 1, f, :, Q_HALF:], lhsT=ident_bf[:], rhs=quads[:, 1, :, Q_HALF:, f, :], start=True, stop=True
@@ -115,43 +116,43 @@ def tile_gptossmlaattention_pb_kernel(tc, hidden_states, cos, sin, Wq, bq, grad_
                 )
             return bank
 
-        def products_of(a, r0, n, bank):
-            products = wide.tile([P, 2, HEADS, 2, PAIR, HALF], F32)
-            quads = rows_of_chunk(a, r0, n).rearrange("p h (r q f e) -> p h r q f e", r=n, f=2, e=2)
-            places = products[:].rearrange("p x h f r (q e) -> p x h f r q e", e=2)[:, :, :, :, 0:n]
-            tabled = bank[:].rearrange("p x f r (q e) -> p x f r q e", e=2)[:, :, :, r0 : r0 + n]
+        def multiply_by_tables(unit, products, bank, f, h0=0, h1=HEADS):
+            a, r0, n = unit
+            rows = grads[a][:, h0:h1, r0 * HEAD : (r0 + n) * HEAD]
+            quads = rows.rearrange("p h (r q f e) -> p h r q f e", r=n, f=2, e=2)[:, :, :, Q_NOPE:, f, :]
+            places = products[:, :, h0:h1, f].rearrange("p x h r (q e) -> p x h r q e", e=2)[:, :, :, 0:n]
+            tabled = bank[:, :, f].rearrange("p x r (q e) -> p x r q e", e=2)[:, :, r0 : r0 + n]
 
-            def multiply_quads(f, x, out_q, in_q, table_q):
-                count_q = out_q[1]
+            def multiply_quads(x, count_q, out_q, in_q):
                 nc.vector.tensor_tensor(
-                    out=places[:, x, :, f, :, out_q[0] : out_q[0] + count_q],
-                    in0=quads[:, :, :, Q_NOPE + in_q : Q_NOPE + in_q + count_q, f, :],
-                    in1=tabled[:, x, f, :, table_q : table_q + count_q]
+                    out=places[:, x, :, :, out_q : out_q + count_q],
+                    in0=quads[:, :, :, in_q : in_q + count_q],
+                    in1=tabled[:, x, :, in_q : in_q + count_q]
                     .unsqueeze(1)
-                    .to_broadcast([P, HEADS, n, count_q, 2]),
+                    .to_broadcast([P, h1 - h0, n, count_q, 2]),
                     op=ALU.mult,
                 )
 
-            for f in range(2):
-                multiply_quads(f, 0, (0, 2 * Q_HALF), 0, 0)
-                multiply_quads(f, 1, (0, Q_HALF), Q_HALF, Q_HALF)
-                multiply_quads(f, 1, (Q_HALF, Q_HALF), 0, 0)
-            return products
+            multiply_quads(0, 2 * Q_HALF, 0, 0)
+            multiply_quads(1, Q_HALF, 0, Q_HALF)
+            multiply_quads(1, Q_HALF, Q_HALF, 0)
 
-        def unrotated_of(a, r0, n):
-            gq_rows = wide.tile([P, 2, PAIR, K // 2], BF16)
-            words = rows_of_chunk(a, r0, n).bitcast(F32).rearrange("p h (r q f) -> p h r q f", r=n, f=2)
+        def unrotated_of(unit):
+            a, r0, n = unit
+            gq_rows = wide.tile([P, PARTS, PAIR, K // 2], BF16)
+            rows = grads[a][:, :, r0 * HEAD : (r0 + n) * HEAD]
+            words = rows.bitcast(F32).rearrange("p h (r q f) -> p h r q f", r=n, f=2)
             places = gq_rows[:].bitcast(F32).rearrange("p f r (h q) -> p f h r q", h=HEADS)
-            for f in range(2):
+            for f in range(PARTS):
                 nc.scalar.copy(out=places[:, f, :, 0:n, 0:Q_NOPE], in_=words[:, :, :, 0:Q_NOPE, f])
             return gq_rows
 
-        def add_terms(engine, n, products, gq_rows):
-            places = gq_rows[:].rearrange("p f r (h j) -> p h f r j", h=HEADS)
+        def add_terms(engine, n, products, gq_rows, f, h0=0, h1=HEADS):
+            places = gq_rows[:].rearrange("p f r (h j) -> p f h r j", h=HEADS)
             engine.tensor_tensor(
-                out=places[:, :, :, 0:n, 2 * Q_NOPE :],
-                in0=products[:, 0, :, :, 0:n],
-                in1=products[:, 1, :, :, 0:n],
+                out=places[:, f, h0:h1, 0:n, 2 * Q_NOPE :],
+                in0=products[:, 0, h0:h1, f, 0:n],
+                in1=products[:, 1, h0:h1, f, 0:n],
                 op=ALU.add,
             )
 
@@ -160,8 +161,8 @@ def tile_gptossmlaattention_pb_kernel(tc, hidden_states, cos, sin, Wq, bq, grad_
             gq_words = gq_rows[:].bitcast(F32)
             for c in range(PASSES):
                 bank = turned.tile([P, 2, n * P], F32, tag="turned")
-                for i in range(n):
-                    for f in range(2):
+                for f in range(PARTS):
+                    for i in range(n):
                         nc.tensor.transpose(
                             bank[:, f, i * P : (i + 1) * P], gq_words[:, f, i, P * c : P * (c + 1)], ident[:]
                         )
@@ -171,8 +172,8 @@ def tile_gptossmlaattention_pb_kernel(tc, hidden_states, cos, sin, Wq, bq, grad_
             return gq_grouped
 
         def quantise_tokens(n, gq_grouped):
-            gq_codes = stage.tile([P, PASSES, PAIR * P], U32, align_bytes=64)
-            gq_scales = stage.tile([P, PASSES, PAIR * P], U8, align_bytes=64)
+            gq_codes = coded.tile([P, PASSES, PAIR * P], U32, align_bytes=64)
+            gq_scales = coded.tile([P, PASSES, PAIR * P], U8, align_bytes=64)
             for c in range(PASSES):
                 nc.vector.quantize_mx(
                     out=gq_codes[:, c, 0 : n * P].bitcast(E5M2X4),
@@ -181,40 +182,17 @@ def tile_gptossmlaattention_pb_kernel(tc, hidden_states, cos, sin, Wq, bq, grad_
                 )
             return gq_codes, gq_scales
 
-        def multiply(a, r0, n, gq_codes, gq_scales, last):
-            result = results.tile([P, PAIR, HID], F32)
-            for i in range(n):
-                rows = slice(i * P, (i + 1) * P)
-                for half in range(N_HALVES):
-                    cols = slice(half * N_TILE, (half + 1) * N_TILE)
-                    acc = sums.tile([P, N_TILE], F32)
-                    for c in range(PASSES):
-                        nc.tensor.matmul_mx(
-                            out=acc[:],
-                            lhsT=gq_codes[:, c, rows].bitcast(E5M2X4),
-                            lhsT_scale=gq_scales[:, c, rows],
-                            rhs=w_codes[:, c, cols].bitcast(E4M3X4),
-                            rhs_scale=w_scales[:, c, cols],
-                            start=(c == 0),
-                            stop=(c == PASSES - 1),
-                        )
-                    nc.scalar.copy(out=result[:, i, cols], in_=acc[:])
-                    if last:
-                        nc.sync.dma_start(out=out_rows[a][:, r0 + i, cols], in_=result[:, i, cols])
-            if not last:
-                nc.sync.dma_start(out=out_rows[a][:, r0 : r0 + n, :], in_=result[:, 0:n, :])
-
-        singles = (0, CHUNKS - 2, CHUNKS - 1)
-        units = []
-        for a in range(CHUNKS):
-            units.extend([(a, r, 1) for r in range(PAIR)] if a in singles else [(a, 0, PAIR)])
-        count = len(units)
-        adders = [nc.gpsimd] * (count - 1) + [nc.vector]
-
         w_grouped = keep.tile([P, PASSES, HID, PACK], BF16, align_bytes=64)
         w_codes = keep.tile([P, PASSES, HID], U32, align_bytes=64)
         w_scales = keep.tile([P, PASSES, HID], U8, align_bytes=64)
         w_words = w_rows[:].bitcast(F32)
+
+        def turn_w(q):
+            for c in range(PASSES):
+                turn(
+                    [w_words[:, PAIR * q + j, :] for j in range(PAIR)], c,
+                    w_grouped[:, c, PAIR * P * q : PAIR * P * (q + 1), :],
+                )
 
         def quantise_w(half):
             cols = slice(N_TILE * half, N_TILE * (half + 1))
@@ -225,46 +203,145 @@ def tile_gptossmlaattention_pb_kernel(tc, hidden_states, cos, sin, Wq, bq, grad_
                     in_=w_grouped[:, c, cols, :].rearrange("p n t -> p (n t)"),
                 )
 
-        def turn_w(q):
-            for c in range(PASSES):
-                turn(
-                    [w_words[:, PAIR * q + j, :] for j in range(PAIR)], c,
-                    w_grouped[:, c, PAIR * P * q : PAIR * P * (q + 1), :],
-                )
+        def multiply_pass(acc, codes, i, half, c):
+            rows = slice(i * P, (i + 1) * P)
+            cols = slice(half * N_TILE, (half + 1) * N_TILE)
+            nc.tensor.matmul_mx(
+                out=acc[:],
+                lhsT=codes[0][:, c, rows].bitcast(E5M2X4),
+                lhsT_scale=codes[1][:, c, rows],
+                rhs=w_codes[:, c, cols].bitcast(E4M3X4),
+                rhs_scale=w_scales[:, c, cols],
+                start=(c == 0),
+                stop=(c == PASSES - 1),
+            )
 
         def hold_gpsimd(read_by_quantise):
             nc.gpsimd.memset(read_by_quantise, 0.0)
 
-        banks = {a: tables_to_psum(a) for a in range(2)}
-        products = {}
+        units = [(a, 0, PAIR) for a in range(CHUNKS - 1)] + [(CHUNKS - 1, r, 1) for r in range(PAIR)]
+        count = len(units)
+        last_pair = CHUNKS - 2
+        added_by_vector = (last_pair, count - 1)
+
+        banks = {}
+        products_of = {}
         rows_of = {}
         grouped_of = {}
         codes_of = {}
-        for s in range(count + 3):
-            if s + 1 < count and units[s + 1][0] not in banks:
-                banks[units[s + 1][0]] = tables_to_psum(units[s + 1][0])
-            for u in {0: [0, 1, 2], 1: [], 2: []}.get(s, [s]):
-                if u < count:
-                    rows_of[u] = unrotated_of(units[u][0], units[u][1], units[u][2])
-            if s < count:
-                a, r0, n = units[s]
-                products[s] = products_of(a, r0, n, banks[a])
-            if s == 0:
-                turn_w(0)
-                turn_w(1)
-            if 0 <= s - 1 < count:
-                add_terms(adders[s - 1], units[s - 1][2], products[s - 1], rows_of[s - 1])
+        result_of = {}
+        stored = {}
+
+        def tables_for(u):
+            if u < count and units[u][0] not in banks:
+                banks[units[u][0]] = tables_to_psum(units[u][0])
+
+        def products(u, part):
+            if u >= count:
+                return
+            if part == 0:
+                fresh = wide.tile([P, 2, HEADS, PARTS, PAIR, HALF], F32, name="products")
+                products_of[u] = fresh
+            bank = banks[units[u][0]]
+            if u == 0:
+                for f in range(PARTS):
+                    multiply_by_tables(units[u], products_of[u], bank, f, part * HEADS // 2, (part + 1) * HEADS // 2)
+            else:
+                multiply_by_tables(units[u], products_of[u], bank, part)
+
+        def add(u, part, engine):
+            if not 0 <= u < count:
+                return
+            n = units[u][2]
+            if u == 0:
+                for f in range(PARTS):
+                    add_terms(engine, n, products_of[u], rows_of[u], f, part * HEADS // 2, (part + 1) * HEADS // 2)
+            else:
+                add_terms(engine, n, products_of[u], rows_of[u], part)
+
+        def unrotated(u):
+            if u < count:
+                rows_of[u] = unrotated_of(units[u])
+
+        def turn_unit(u):
+            if 0 <= u < count:
+                grouped_of[u] = turn_tokens(units[u][2], rows_of[u])
+
+        def quantise_unit(u):
+            if 0 <= u < count:
+                codes_of[u] = quantise_tokens(units[u][2], grouped_of[u])
+                hold_gpsimd(grouped_of[u][:, PASSES - 2, 0, 0:2])
+
+        def tiles_of(u):
+            return [(u, i, half) for i in range(units[u][2]) for half in range(N_HALVES)] if 0 <= u < count else []
+
+        def multiply(jobs):
+            for u, i, half in jobs:
+                a, r0, n = units[u]
+                if u not in result_of:
+                    fresh = results.tile([P, PAIR, HID], F32, name="result")
+                    result_of[u] = fresh
+                    stored[u] = 0
+                acc = sums.tile([P, N_TILE], F32)
+                for c in range(PASSES):
+                    multiply_pass(acc, codes_of[u], i, half, c)
+                nc.scalar.copy(out=result_of[u][:, i, half * N_TILE : (half + 1) * N_TILE], in_=acc[:])
+                stored[u] += 1
+                if stored[u] == n * N_HALVES:
+                    nc.sync.dma_start(out=out_rows[a][:, r0 : r0 + n, :], in_=result_of[u][:, 0:n, :])
+
+        def multiply_last():
+            u = count - 1
+            a, r0, n = units[u]
+            result = results.tile([P, PAIR, HID], F32, name="result")
+            accs = []
+            for half in range(N_HALVES):
+                acc = sums.tile([P, N_TILE], F32)
+                accs.append(acc)
+            for c in range(PASSES):
+                for half in range(N_HALVES):
+                    multiply_pass(accs[half], codes_of[u], 0, half, c)
+            for half, copy in enumerate((nc.scalar.copy, nc.vector.tensor_copy)):
+                cols = slice(half * N_TILE, (half + 1) * N_TILE)
+                copy(out=result[:, 0, cols], in_=accs[half][:])
+                nc.sync.dma_start(out=out_rows[a][:, r0, cols], in_=result[:, 0, cols])
+
+        runs = {s: (tiles_of(s - 2)[0:2], tiles_of(s - 2)[2:]) for s in range(count + 1)}
+        runs[2] = ([], [(0, 0, 0), (0, 1, 0)])
+        runs[3] = ([(1, 0, 0), (1, 1, 0)], [(0, 0, 1), (0, 1, 1), (1, 0, 1), (1, 1, 1)])
+        tables_for(0)
+        tables_for(1)
+        unrotated(0)
+        for s in range(count):
+            products(s, 0)
+            tables_for(s + 1)
+            if s >= 1 and s - 1 not in added_by_vector:
+                add(s - 1, 1, nc.gpsimd)
             if s == 2:
-                quantise_w(0)
-            if 0 <= s - 2 < count:
-                grouped_of[s - 2] = turn_tokens(units[s - 2][2], rows_of[s - 2])
-            if s == 3:
+                quantise_unit(0)
+            if s in (2, 3):
+                quantise_w(s - 2)
+                hold_gpsimd(w_grouped[:, PASSES - 2, (s - 2) * N_TILE, 0:2])
+            multiply(runs[s][0])
+            products(s, 1)
+            add(s, 0, nc.gpsimd)
+            if s == 0:
+                unrotated(1)
+                turn_w(0)
+            turn_unit(s - 1)
+            if s == 1:
+                turn_w(1)
                 turn_w(2)
+            if s == 2:
                 turn_w(3)
-                quantise_w(1)
-            if 0 <= s - 3 < count:
-                a, r0, n = units[s - 3]
-                multiply(a, r0, n, codes_of[s - 3][0], codes_of[s - 3][1], s - 3 == count - 1)
-            if 0 <= s - 2 < count:
-                codes_of[s - 2] = quantise_tokens(units[s - 2][2], grouped_of[s - 2])
-                hold_gpsimd(grouped_of[s - 2][:, PASSES - 2, 0, 0:2])
+            if s >= 1:
+                unrotated(s + 1)
+            multiply(runs[s][1])
+            if s != 1:
+                quantise_unit(s - 1)
+            if s in added_by_vector:
+                add(s, 1, nc.vector)
+        turn_unit(count - 1)
+        multiply(tiles_of(count - 2))
+        quantise_unit(count - 1)
+        multiply_last()

@@ -79,9 +79,9 @@ def tile_gptossmlaattention_pb_kernel(tc, hidden_states, cos, sin, Wq, bq, grad_
         load_grads(0, HEADS // 2, HEADS)
         load_grads(1)
         load_w(0)
-        load_w(1)
         load_tables(2, 4)
         load_grads(2)
+        load_w(1)
         load_w(2)
         load_w(3)
         load_tables(4, CHUNKS)
@@ -270,7 +270,7 @@ def tile_gptossmlaattention_pb_kernel(tc, hidden_states, cos, sin, Wq, bq, grad_
         def quantise_unit(u):
             if 0 <= u < count:
                 codes_of[u] = quantise_tokens(units[u][2], grouped_of[u])
-                hold_gpsimd(grouped_of[u][:, PASSES - 2, 0, 0:2])
+                hold_gpsimd(grouped_of[u][:, 0 if u < last_pair else PASSES - 2, 0, 0:2])
 
         def tiles_of(u):
             return [(u, i, half) for i in range(units[u][2]) for half in range(N_HALVES)] if 0 <= u < count else []

@@ -116,7 +116,7 @@ def tile_gptossmlaattention_pb_kernel(tc, hidden_states, cos, sin, Wq, bq, grad_
                 )
             return bank
 
-        def multiply_by_tables(unit, products, bank, f, h0=0, h1=HEADS):
+        def multiply_by_tables(unit, products, bank, f, terms, h0=0, h1=HEADS):
             a, r0, n = unit
             rows = grads[a][:, h0:h1, r0 * HEAD : (r0 + n) * HEAD]
             quads = rows.rearrange("p h (r q f e) -> p h r q f e", r=n, f=2, e=2)[:, :, :, Q_NOPE:, f, :]
@@ -133,9 +133,12 @@ def tile_gptossmlaattention_pb_kernel(tc, hidden_states, cos, sin, Wq, bq, grad_
                     op=ALU.mult,
                 )
 
-            multiply_quads(0, 2 * Q_HALF, 0, 0)
-            multiply_quads(1, Q_HALF, 0, Q_HALF)
-            multiply_quads(1, Q_HALF, Q_HALF, 0)
+            for x, count_q, out_q, in_q in terms:
+                multiply_quads(x, count_q, out_q, in_q)
+
+        COS = (0, 2 * Q_HALF, 0, 0)
+        SIN_FIRST = (1, Q_HALF, 0, Q_HALF)
+        SIN_SECOND = (1, Q_HALF, Q_HALF, 0)
 
         def unrotated_of(unit):
             a, r0, n = unit
@@ -216,9 +219,6 @@ def tile_gptossmlaattention_pb_kernel(tc, hidden_states, cos, sin, Wq, bq, grad_
                 stop=(c == PASSES - 1),
             )
 
-        def hold_gpsimd(read_by_quantise):
-            nc.gpsimd.memset(read_by_quantise, 0.0)
-
         units = [(a, 0, PAIR) for a in range(CHUNKS - 1)] + [(CHUNKS - 1, r, 1) for r in range(PAIR)]
         count = len(units)
         last_pair = CHUNKS - 2
@@ -236,7 +236,7 @@ def tile_gptossmlaattention_pb_kernel(tc, hidden_states, cos, sin, Wq, bq, grad_
             if u < count and units[u][0] not in banks:
                 banks[units[u][0]] = tables_to_psum(units[u][0])
 
-        def products(u, part):
+        def products(u, part, held_back=False):
             if u >= count:
                 return
             if part == 0:
@@ -245,9 +245,20 @@ def tile_gptossmlaattention_pb_kernel(tc, hidden_states, cos, sin, Wq, bq, grad_
             bank = banks[units[u][0]]
             if u == 0:
                 for f in range(PARTS):
-                    multiply_by_tables(units[u], products_of[u], bank, f, part * HEADS // 2, (part + 1) * HEADS // 2)
+                    multiply_by_tables(
+                        units[u], products_of[u], bank, f, (COS, SIN_FIRST, SIN_SECOND),
+                        part * HEADS // 2, (part + 1) * HEADS // 2,
+                    )
+            elif held_back:
+                multiply_by_tables(units[u], products_of[u], bank, part, (COS, SIN_FIRST))
+                multiply_by_tables(units[u], products_of[u], bank, part, (SIN_SECOND,), 0, HEADS - 1)
             else:
-                multiply_by_tables(units[u], products_of[u], bank, part)
+                multiply_by_tables(units[u], products_of[u], bank, part, (COS, SIN_FIRST, SIN_SECOND))
+
+        def rest_of_products(u, part):
+            multiply_by_tables(
+                units[u], products_of[u], banks[units[u][0]], part, (SIN_SECOND,), HEADS - 1, HEADS
+            )
 
         def add(u, part, engine):
             if not 0 <= u < count:
@@ -270,7 +281,6 @@ def tile_gptossmlaattention_pb_kernel(tc, hidden_states, cos, sin, Wq, bq, grad_
         def quantise_unit(u):
             if 0 <= u < count:
                 codes_of[u] = quantise_tokens(units[u][2], grouped_of[u])
-                hold_gpsimd(grouped_of[u][:, 0 if u < last_pair else PASSES - 2, 0, 0:2])
 
         def tiles_of(u):
             return [(u, i, half) for i in range(units[u][2]) for half in range(N_HALVES)] if 0 <= u < count else []
@@ -313,7 +323,7 @@ def tile_gptossmlaattention_pb_kernel(tc, hidden_states, cos, sin, Wq, bq, grad_
         tables_for(1)
         unrotated(0)
         for s in range(count):
-            products(s, 0)
+            products(s, 0, s in (2, 3))
             tables_for(s + 1)
             if s >= 1 and s - 1 not in added_by_vector:
                 add(s - 1, 1, nc.gpsimd)
@@ -321,9 +331,10 @@ def tile_gptossmlaattention_pb_kernel(tc, hidden_states, cos, sin, Wq, bq, grad_
                 quantise_unit(0)
             if s in (2, 3):
                 quantise_w(s - 2)
-                hold_gpsimd(w_grouped[:, PASSES - 2, (s - 2) * N_TILE, 0:2])
+                rest_of_products(s, 0)
             multiply(runs[s][0])
-            products(s, 1)
+            hold = s >= 2 and s not in added_by_vector
+            products(s, 1, hold)
             add(s, 0, nc.gpsimd)
             if s == 0:
                 unrotated(1)
@@ -339,6 +350,8 @@ def tile_gptossmlaattention_pb_kernel(tc, hidden_states, cos, sin, Wq, bq, grad_
             multiply(runs[s][1])
             if s != 1:
                 quantise_unit(s - 1)
+            if hold:
+                rest_of_products(s, 1)
             if s in added_by_vector:
                 add(s, 1, nc.vector)
         turn_unit(count - 1)

@@ -56,7 +56,7 @@ def tile_gptossmlaattention_pb_kernel(tc, hidden_states, cos, sin, Wq, bq, grad_
         ident = keep.tile([P, P], F32)
         make_identity(nc, ident[:])
 
-        tables = keep.tile([P, CHUNKS, 2, PAIR * ROPE], BF16)
+        tables = keep.tile([P, 2, CHUNKS, PAIR * ROPE], BF16)
         grads = [keep.tile([P, HEADS, PAIR * HEAD], BF16, name="grads%d" % a) for a in range(CHUNKS)]
         w_rows = keep.tile([P, HID // P, K], BF16)
         grad_chunks = grad_out.rearrange("b h (p a r) d -> a p (b h) (r d)", p=P, r=PAIR)
@@ -66,7 +66,7 @@ def tile_gptossmlaattention_pb_kernel(tc, hidden_states, cos, sin, Wq, bq, grad_
 
         def load_tables(a0, a1):
             for x in range(2):
-                nc.sync.dma_start(out=tables[:, a0:a1, x], in_=table_views[x][:, a0:a1])
+                nc.sync.dma_start(out=tables[:, x, a0:a1], in_=table_views[x][:, a0:a1])
 
         def load_grads(a, h0=0, h1=HEADS):
             nc.sync.dma_start(out=grads[a][:, h0:h1], in_=grad_chunks[a][:, h0:h1])
@@ -74,12 +74,12 @@ def tile_gptossmlaattention_pb_kernel(tc, hidden_states, cos, sin, Wq, bq, grad_
         def load_w(q):
             nc.sync.dma_start(out=w_rows[:, PAIR * q : PAIR * (q + 1), :], in_=w_view[:, PAIR * q : PAIR * (q + 1), :])
 
-        load_tables(0, 2)
+        load_tables(0, 1)
         load_grads(0, 0, HEADS // 2)
         load_grads(0, HEADS // 2, HEADS)
+        load_tables(1, 4)
         load_grads(1)
         load_w(0)
-        load_tables(2, 4)
         load_grads(2)
         load_w(1)
         load_w(2)
@@ -103,7 +103,7 @@ def tile_gptossmlaattention_pb_kernel(tc, hidden_states, cos, sin, Wq, bq, grad_
 
         def tables_to_psum(a):
             bank = spread.tile([P, 2, PARTS, PAIR, HALF], F32)
-            quads = tables[:, a].rearrange("p x (r q f e) -> p x r q f e", r=PAIR, f=2, e=2)
+            quads = tables[:, :, a].rearrange("p x (r q f e) -> p x r q f e", r=PAIR, f=2, e=2)
             places = bank[:].rearrange("p x f r (q e) -> p x f r q e", e=2)
             for f in range(PARTS):
                 nc.tensor.matmul(places[:, 0, f], lhsT=ident_bf[:], rhs=quads[:, 0, :, :, f, :], start=True, stop=True)
@@ -297,7 +297,9 @@ def tile_gptossmlaattention_pb_kernel(tc, hidden_states, cos, sin, Wq, bq, grad_
                     multiply_pass(acc, codes_of[u], i, half, c)
                 nc.scalar.copy(out=result_of[u][:, i, half * N_TILE : (half + 1) * N_TILE], in_=acc[:])
                 stored[u] += 1
-                if stored[u] == n * N_HALVES:
+                if u == last_pair and stored[u] % N_HALVES == 0:
+                    nc.sync.dma_start(out=out_rows[a][:, i, :], in_=result_of[u][:, i, :])
+                elif u != last_pair and stored[u] == n * N_HALVES:
                     nc.sync.dma_start(out=out_rows[a][:, r0 : r0 + n, :], in_=result_of[u][:, 0:n, :])
 
         def multiply_last():
@@ -324,7 +326,6 @@ def tile_gptossmlaattention_pb_kernel(tc, hidden_states, cos, sin, Wq, bq, grad_
         unrotated(0)
         for s in range(count):
             products(s, 0, s in (2, 3))
-            tables_for(s + 1)
             if s >= 1 and s - 1 not in added_by_vector:
                 add(s - 1, 1, nc.gpsimd)
             if s == 2:
@@ -333,6 +334,7 @@ def tile_gptossmlaattention_pb_kernel(tc, hidden_states, cos, sin, Wq, bq, grad_
                 quantise_w(s - 2)
                 rest_of_products(s, 0)
             multiply(runs[s][0])
+            tables_for(s + 1)
             hold = s >= 2 and s not in added_by_vector
             products(s, 1, hold)
             add(s, 0, nc.gpsimd)
@@ -348,11 +350,13 @@ def tile_gptossmlaattention_pb_kernel(tc, hidden_states, cos, sin, Wq, bq, grad_
             if s >= 1:
                 unrotated(s + 1)
             multiply(runs[s][1])
+            if s == count - 1:
+                add(s, 1, nc.vector)
             if s != 1:
                 quantise_unit(s - 1)
             if hold:
                 rest_of_products(s, 1)
-            if s in added_by_vector:
+            if s == last_pair:
                 add(s, 1, nc.vector)
         turn_unit(count - 1)
         multiply(tiles_of(count - 2))

@@ -77,16 +77,20 @@ def tile_gptossmlaattention_pb_kernel(tc, hidden_states, cos, sin, Wq, bq, grad_
         load_tables(0, 1)
         load_grads(0, 0, HEADS // 2)
         load_grads(0, HEADS // 2, HEADS)
-        load_tables(1, 4)
+        load_tables(1, 2)
         load_grads(1)
         load_w(0)
+        load_tables(2, 4)
         load_grads(2)
         load_w(1)
         load_w(2)
         load_w(3)
-        load_tables(4, CHUNKS)
-        for a in range(3, CHUNKS):
-            load_grads(a)
+        load_grads(3)
+        load_tables(4, 8)
+        load_grads(4)
+        load_grads(5)
+        load_grads(6)
+        load_grads(7)
 
         def turn(row_words, c, grouped):
             n = len(row_words)
@@ -320,28 +324,42 @@ def tile_gptossmlaattention_pb_kernel(tc, hidden_states, cos, sin, Wq, bq, grad_
 
         runs = {s: (tiles_of(s - 2)[0:2], tiles_of(s - 2)[2:]) for s in range(count + 1)}
         runs[2] = ([], [(0, 0, 0), (0, 1, 0)])
-        runs[3] = ([(1, 0, 0), (1, 1, 0)], [(0, 0, 1), (0, 1, 1), (1, 0, 1), (1, 1, 1)])
+        runs[3] = ([], [(1, 0, 0), (1, 1, 0), (0, 0, 1), (0, 1, 1)])
+        runs[4] = ([(1, 0, 1), (1, 1, 1)], tiles_of(2)[0:2])
+        runs[5] = (tiles_of(2)[2:], tiles_of(3)[0:2] + tiles_of(3)[2:])
+        runs[6] = (tiles_of(4)[0:2], tiles_of(4)[2:])
+        runs[7] = (tiles_of(5)[0:2], tiles_of(5)[2:])
+        runs[8] = (tiles_of(6)[0:2], tiles_of(6)[2:])
         tables_for(0)
         tables_for(1)
         unrotated(0)
         for s in range(count):
-            products(s, 0, s in (2, 3))
+            mid = s in (2, 3, 4, 5,)
+            products(s, 0, mid)
             if s >= 1 and s - 1 not in added_by_vector:
                 add(s - 1, 1, nc.gpsimd)
             if s == 2:
                 quantise_unit(0)
-            if s in (2, 3):
-                quantise_w(s - 2)
+                quantise_w(0)
+            if s == 3:
+                quantise_unit(1)
+                quantise_w(1)
+            if s == 4:
+                quantise_unit(2)
+            if s == 5:
+                quantise_unit(3)
+            if mid:
                 rest_of_products(s, 0)
             multiply(runs[s][0])
             tables_for(s + 1)
-            hold = s >= 2 and s not in added_by_vector
+            hold = s in (5, 7,)
             products(s, 1, hold)
             add(s, 0, nc.gpsimd)
             if s == 0:
                 unrotated(1)
                 turn_w(0)
-            turn_unit(s - 1)
+            if s not in (99,):
+                turn_unit(s - 1)
             if s == 1:
                 turn_w(1)
                 turn_w(2)
@@ -352,7 +370,7 @@ def tile_gptossmlaattention_pb_kernel(tc, hidden_states, cos, sin, Wq, bq, grad_
             multiply(runs[s][1])
             if s == count - 1:
                 add(s, 1, nc.vector)
-            if s != 1:
+            if s not in (1, 2, 3, 4, 99,):
                 quantise_unit(s - 1)
             if hold:
                 rest_of_products(s, 1)

@@ -124,25 +124,18 @@ def tile_gptossmlaattention_pb_kernel(tc, hidden_states, cos, sin, Wq, bq, grad_
             a, r0, n = unit
             rows = grads[a][:, h0:h1, r0 * HEAD : (r0 + n) * HEAD]
             quads = rows.rearrange("p h (r q f e) -> p h r q f e", r=n, f=2, e=2)[:, :, :, Q_NOPE:, f, :]
-            places = products[:, :, h0:h1, f].rearrange("p x h r (q e) -> p x h r q e", e=2)[:, :, :, 0:n]
+            places = products[:, :, f, h0:h1].rearrange("p x h r (q e) -> p x h r q e", e=2)[:, :, :, 0:n]
             tabled = bank[:, :, f].rearrange("p x r (q e) -> p x r q e", e=2)[:, :, r0 : r0 + n]
 
-            def multiply_quads(x, count_q, out_q, in_q):
+            for x in terms:
                 nc.vector.tensor_tensor(
-                    out=places[:, x, :, :, out_q : out_q + count_q],
-                    in0=quads[:, :, :, in_q : in_q + count_q],
-                    in1=tabled[:, x, :, in_q : in_q + count_q]
-                    .unsqueeze(1)
-                    .to_broadcast([P, h1 - h0, n, count_q, 2]),
+                    out=places[:, x],
+                    in0=quads,
+                    in1=tabled[:, x].unsqueeze(1).to_broadcast([P, h1 - h0, n, 2 * Q_HALF, 2]),
                     op=ALU.mult,
                 )
 
-            for x, count_q, out_q, in_q in terms:
-                multiply_quads(x, count_q, out_q, in_q)
-
-        COS = (0, 2 * Q_HALF, 0, 0)
-        SIN_FIRST = (1, Q_HALF, 0, Q_HALF)
-        SIN_SECOND = (1, Q_HALF, Q_HALF, 0)
+        COS, SIN = 0, 1
 
         def unrotated_of(unit):
             a, r0, n = unit
@@ -157,9 +150,9 @@ def tile_gptossmlaattention_pb_kernel(tc, hidden_states, cos, sin, Wq, bq, grad_
         def add_terms(engine, n, products, gq_rows, f, h0=0, h1=HEADS):
             places = gq_rows[:].rearrange("p f r (h j) -> p f h r j", h=HEADS)
             engine.tensor_tensor(
-                out=places[:, f, h0:h1, 0:n, 2 * Q_NOPE :],
-                in0=products[:, 0, h0:h1, f, 0:n],
-                in1=products[:, 1, h0:h1, f, 0:n],
+                out=places[:, f, h0:h1, 0:n, 2 * Q_NOPE :].rearrange("p h r (j k) -> p h r j k", j=2),
+                in0=products[:, 0, f, h0:h1, 0:n].rearrange("p h r (j k) -> p h r j k", j=2),
+                in1=products[:, 1, f, h0:h1, 0:n].rearrange("p h r (j k) -> p h r j k", j=2)[:, :, :, ::-1],
                 op=ALU.add,
             )
 
@@ -178,10 +171,12 @@ def tile_gptossmlaattention_pb_kernel(tc, hidden_states, cos, sin, Wq, bq, grad_
                 )
             return gq_grouped
 
-        def quantise_tokens(n, gq_grouped):
+        def quantise_tokens(n, gq_grouped, before_last):
             gq_codes = coded.tile([P, PASSES, PAIR * P], U32, align_bytes=64)
             gq_scales = coded.tile([P, PASSES, PAIR * P], U8, align_bytes=64)
             for c in range(PASSES):
+                if c == PASSES - 1:
+                    before_last()
                 nc.vector.quantize_mx(
                     out=gq_codes[:, c, 0 : n * P].bitcast(E5M2X4),
                     scales=gq_scales[:, c, 0 : n * P],
@@ -201,9 +196,11 @@ def tile_gptossmlaattention_pb_kernel(tc, hidden_states, cos, sin, Wq, bq, grad_
                     w_grouped[:, c, PAIR * P * q : PAIR * P * (q + 1), :],
                 )
 
-        def quantise_w(half):
+        def quantise_w(half, before_last=lambda: None):
             cols = slice(N_TILE * half, N_TILE * (half + 1))
             for c in range(PASSES):
+                if c == PASSES - 1:
+                    before_last()
                 nc.vector.quantize_mx(
                     out=w_codes[:, c, cols].bitcast(E4M3X4),
                     scales=w_scales[:, c, cols],
@@ -244,27 +241,27 @@ def tile_gptossmlaattention_pb_kernel(tc, hidden_states, cos, sin, Wq, bq, grad_
             if u >= count:
                 return
             if part == 0:
-                fresh = wide.tile([P, 2, HEADS, PARTS, PAIR, HALF], F32, name="products")
+                fresh = wide.tile([P, 2, PARTS, HEADS, PAIR, HALF], F32, name="products")
                 products_of[u] = fresh
             bank = banks[units[u][0]]
             if u == 0:
                 for f in range(PARTS):
                     multiply_by_tables(
-                        units[u], products_of[u], bank, f, (COS, SIN_FIRST, SIN_SECOND),
+                        units[u], products_of[u], bank, f, (COS, SIN),
                         part * HEADS // 2, (part + 1) * HEADS // 2,
                     )
             elif held_back:
-                multiply_by_tables(units[u], products_of[u], bank, part, (COS, SIN_FIRST))
-                multiply_by_tables(units[u], products_of[u], bank, part, (SIN_SECOND,), 0, HEADS - 1)
+                multiply_by_tables(units[u], products_of[u], bank, part, (COS,))
+                multiply_by_tables(units[u], products_of[u], bank, part, (SIN,), 1, HEADS)
             else:
-                multiply_by_tables(units[u], products_of[u], bank, part, (COS, SIN_FIRST, SIN_SECOND))
+                multiply_by_tables(units[u], products_of[u], bank, part, (COS, SIN))
 
         def rest_of_products(u, part):
             multiply_by_tables(
-                units[u], products_of[u], banks[units[u][0]], part, (SIN_SECOND,), HEADS - 1, HEADS
+                units[u], products_of[u], banks[units[u][0]], part, (SIN,), 0, 1
             )
 
-        def add(u, part, engine):
+        def add(u, part, engine, h0=0, h1=HEADS):
             if not 0 <= u < count:
                 return
             n = units[u][2]
@@ -272,7 +269,7 @@ def tile_gptossmlaattention_pb_kernel(tc, hidden_states, cos, sin, Wq, bq, grad_
                 for f in range(PARTS):
                     add_terms(engine, n, products_of[u], rows_of[u], f, part * HEADS // 2, (part + 1) * HEADS // 2)
             else:
-                add_terms(engine, n, products_of[u], rows_of[u], part)
+                add_terms(engine, n, products_of[u], rows_of[u], part, h0, h1)
 
         def unrotated(u):
             if u < count:
@@ -282,9 +279,9 @@ def tile_gptossmlaattention_pb_kernel(tc, hidden_states, cos, sin, Wq, bq, grad_
             if 0 <= u < count:
                 grouped_of[u] = turn_tokens(units[u][2], rows_of[u])
 
-        def quantise_unit(u):
+        def quantise_unit(u, before_last=lambda: None):
             if 0 <= u < count:
-                codes_of[u] = quantise_tokens(units[u][2], grouped_of[u])
+                codes_of[u] = quantise_tokens(units[u][2], grouped_of[u], before_last)
 
         def tiles_of(u):
             return [(u, i, half) for i in range(units[u][2]) for half in range(N_HALVES)] if 0 <= u < count else []
@@ -337,18 +334,20 @@ def tile_gptossmlaattention_pb_kernel(tc, hidden_states, cos, sin, Wq, bq, grad_
             mid = s in (2, 3, 4, 5,)
             products(s, 0, mid)
             if s >= 1 and s - 1 not in added_by_vector:
-                add(s - 1, 1, nc.gpsimd)
+                add(s - 1, 1, nc.gpsimd, 0, 6 if s in (3, 4, 5, 6,) else HEADS)
+            if s in (3, 4, 5, 6,):
+                add(s - 1, 1, nc.vector, 6, HEADS)
             if s == 2:
                 quantise_unit(0)
                 quantise_w(0)
             if s == 3:
                 quantise_unit(1)
-                quantise_w(1)
+                quantise_w(1, lambda: rest_of_products(3, 0))
             if s == 4:
-                quantise_unit(2)
+                quantise_unit(2, lambda: rest_of_products(4, 0))
             if s == 5:
-                quantise_unit(3)
-            if mid:
+                quantise_unit(3, lambda: rest_of_products(5, 0))
+            if mid and s not in (3, 4, 5,):
                 rest_of_products(s, 0)
             multiply(runs[s][0])
             tables_for(s + 1)

@@ -220,9 +220,11 @@ def tile_gptossmlaattention_pb_kernel(tc, hidden_states, cos, sin, Wq, bq, grad_
                 stop=(c == PASSES - 1),
             )
 
-        units = [(a, 0, PAIR) for a in range(CHUNKS - 1)] + [(CHUNKS - 1, r, 1) for r in range(PAIR)]
+        units = []
+        for a in range(CHUNKS):
+            units.extend([(a, r, 1) for r in range(PAIR)] if a in (CHUNKS - 2, CHUNKS - 1) else [(a, 0, PAIR)])
         count = len(units)
-        last_pair = CHUNKS - 2
+        last_pair = max([-1] + [u for u in range(count - 1) if units[u][2] == PAIR])
         added_by_vector = (last_pair, count - 1)
 
         banks = {}
@@ -320,22 +322,26 @@ def tile_gptossmlaattention_pb_kernel(tc, hidden_states, cos, sin, Wq, bq, grad_
                 nc.sync.dma_start(out=out_rows[a][:, r0, cols], in_=result[:, 0, cols])
 
         runs = {s: (tiles_of(s - 2)[0:2], tiles_of(s - 2)[2:]) for s in range(count + 1)}
+        half = {u: len(tiles_of(u)) // 2 for u in range(count)}
+        runs = {}
+        for s in range(count):
+            first = tiles_of(s - 3)[half[s - 3]:] if s >= 5 else []
+            second = tiles_of(s - 2)[0:half[s - 2]] if s >= 4 else []
+            if s == count - 1:
+                second = tiles_of(s - 2)[0:3]
+            runs[s] = (first, second)
         runs[2] = ([], [(0, 0, 0), (0, 1, 0)])
         runs[3] = ([], [(1, 0, 0), (1, 1, 0), (0, 0, 1), (0, 1, 1)])
-        runs[4] = ([(1, 0, 1), (1, 1, 1)], tiles_of(2)[0:2])
-        runs[5] = (tiles_of(2)[2:], tiles_of(3)[0:2] + tiles_of(3)[2:])
-        runs[6] = (tiles_of(4)[0:2], tiles_of(4)[2:])
-        runs[7] = (tiles_of(5)[0:2], tiles_of(5)[2:])
-        runs[8] = (tiles_of(6)[0:2], tiles_of(6)[2:])
+        runs[4] = ([(1, 0, 1), (1, 1, 1)], runs[4][1])
         tables_for(0)
         tables_for(1)
         unrotated(0)
         for s in range(count):
-            mid = s in (2, 3, 4, 5,)
+            mid = s >= 2
             products(s, 0, mid)
             if s >= 1 and s - 1 not in added_by_vector:
-                add(s - 1, 1, nc.gpsimd, 0, 6 if s in (3, 4, 5, 6,) else HEADS)
-            if s in (3, 4, 5, 6,):
+                add(s - 1, 1, nc.gpsimd, 0, 6 if 3 <= s <= 5 else HEADS)
+            if 3 <= s <= 5:
                 add(s - 1, 1, nc.vector, 6, HEADS)
             if s == 2:
                 quantise_unit(0)
@@ -343,15 +349,13 @@ def tile_gptossmlaattention_pb_kernel(tc, hidden_states, cos, sin, Wq, bq, grad_
             if s == 3:
                 quantise_unit(1)
                 quantise_w(1, lambda: rest_of_products(3, 0))
-            if s == 4:
-                quantise_unit(2, lambda: rest_of_products(4, 0))
-            if s == 5:
-                quantise_unit(3, lambda: rest_of_products(5, 0))
-            if mid and s not in (3, 4, 5,):
+            if s >= 4:
+                quantise_unit(s - 2, lambda: rest_of_products(s, 0))
+            if s == 2:
                 rest_of_products(s, 0)
             multiply(runs[s][0])
             tables_for(s + 1)
-            hold = s in (5, 7,)
+            hold = False
             products(s, 1, hold)
             add(s, 0, nc.gpsimd)
             if s == 0:
@@ -369,13 +373,13 @@ def tile_gptossmlaattention_pb_kernel(tc, hidden_states, cos, sin, Wq, bq, grad_
             multiply(runs[s][1])
             if s == count - 1:
                 add(s, 1, nc.vector)
-            if s not in (1, 2, 3, 4, 99,):
+            if s == count - 1:
                 quantise_unit(s - 1)
             if hold:
                 rest_of_products(s, 1)
             if s == last_pair:
                 add(s, 1, nc.vector)
         turn_unit(count - 1)
-        multiply(tiles_of(count - 2))
+        multiply(tiles_of(count - 3)[3:] + tiles_of(count - 2))
         quantise_unit(count - 1)
         multiply_last()

from contextlib import ExitStack

import concourse.mybir as mybir
from concourse.masks import make_identity

BF16 = mybir.dt.bfloat16
F32 = mybir.dt.float32
U32 = mybir.dt.uint32
U8 = mybir.dt.uint8
E4M3X4 = mybir.dt.float8_e4m3fn_x4
E5M2X4 = mybir.dt.float8_e5m2_x4
ALU = mybir.AluOpType

P = 128
TOKENS = 2048
HEADS = 8
NOPE = 64
ROPE = 128
HALF = ROPE // 2
HEAD = NOPE + ROPE
K = HEADS * HEAD
HID = 1024
PACK = 4
K_PASS = P * PACK
PASSES = K // K_PASS
N_TILE = 512
N_HALVES = HID // N_TILE
PAIR = 2
CHUNKS = TOKENS // (P * PAIR)
WORDS = K_PASS // 2
Q_NOPE = NOPE // PACK
Q_HALF = HALF // PACK
PARTS = 2

FLOPS = 2 * TOKENS * HID * K
BYTES = 2 * (TOKENS * K + HID * K + 2 * TOKENS * ROPE) + 4 * TOKENS * HID


def tile_gptossmlaattention_pb_kernel(tc, hidden_states, cos, sin, Wq, bq, grad_out, out):
    nc = tc.nc
    with ExitStack() as ctx:
        keep = ctx.enter_context(tc.tile_pool(name="keep", bufs=1))
        stage = ctx.enter_context(tc.tile_pool(name="stage", bufs=2))
        coded = ctx.enter_context(tc.tile_pool(name="coded", bufs=3))
        wide = ctx.enter_context(tc.tile_pool(name="wide", bufs=3))
        results = ctx.enter_context(tc.tile_pool(name="results", bufs=3))
        turned = ctx.enter_context(tc.psum_pool(name="turned", bufs=3))
        sums = ctx.enter_context(tc.psum_pool(name="sums", bufs=3))
        spread = ctx.enter_context(tc.psum_pool(name="spread", bufs=2))
        ctx.enter_context(tc.manual_schedule())

        ident_bf = keep.tile([P, P], BF16)
        make_identity(nc, ident_bf[:])
        minus_ident_bf = keep.tile([P, P], BF16)
        nc.scalar.mul(out=minus_ident_bf[:], in_=ident_bf[:], mul=-1.0)
        ident = keep.tile([P, P], F32)
        make_identity(nc, ident[:])

        tables = keep.tile([P, 2, CHUNKS, PAIR * ROPE], BF16)
        grads = [keep.tile([P, HEADS, PAIR * HEAD], BF16, name="grads%d" % a) for a in range(CHUNKS)]
        w_rows = keep.tile([P, HID // P, K], BF16)
        grad_chunks = grad_out.rearrange("b h (p a r) d -> a p (b h) (r d)", p=P, r=PAIR)
        table_views = [x.rearrange("b (p a r) d -> p (b a) (r d)", p=P, r=PAIR) for x in (cos, sin)]
        w_view = Wq.rearrange("(j p) k -> p j k", p=P)
        out_rows = out.rearrange("b (p a r) n -> a p (b r) n", p=P, r=PAIR)

        def load_tables(a0, a1):
            for x in range(2):
                nc.sync.dma_start(out=tables[:, x, a0:a1], in_=table_views[x][:, a0:a1])

        def load_grads(a, h0=0, h1=HEADS):
            nc.sync.dma_start(out=grads[a][:, h0:h1], in_=grad_chunks[a][:, h0:h1])

        def load_w(q):
            nc.sync.dma_start(out=w_rows[:, PAIR * q : PAIR * (q + 1), :], in_=w_view[:, PAIR * q : PAIR * (q + 1), :])

        load_tables(0, 1)
        load_grads(0, 0, HEADS // 2)
        load_grads(0, HEADS // 2, HEADS)
        load_tables(1, 2)
        load_grads(1)
        load_w(0)
        load_tables(2, 4)
        load_grads(2)
        load_w(1)
        load_w(2)
        load_w(3)
        load_grads(3)
        load_tables(4, 8)
        load_grads(4)
        load_grads(5)
        load_grads(6)
        load_grads(7)

        def turn(row_words, c, grouped):
            n = len(row_words)
            bank = turned.tile([P, 2, n * P], F32, tag="turned")
            for i in range(n):
                for u in range(2):
                    nc.tensor.transpose(
                        bank[:, u, i * P : (i + 1) * P],
                        row_words[i][:, WORDS * c + u : WORDS * (c + 1) : 2],
                        ident[:],
                    )
            nc.scalar.copy(out=grouped.bitcast(F32), in_=bank[:].rearrange("p u n -> p n u"))


        def tables_to_psum(a):
            bank = spread.tile([P, 2, PARTS, PAIR, HALF], F32)
            quads = tables[:, :, a].rearrange("p x (r q f e) -> p x r q f e", r=PAIR, f=2, e=2)
            places = bank[:].rearrange("p x f r (q e) -> p x f r q e", e=2)
            for f in range(PARTS):
                nc.tensor.matmul(places[:, 0, f], lhsT=ident_bf[:], rhs=quads[:, 0, :, :, f, :], start=True, stop=True)
                nc.tensor.matmul(
                    places[:, 1, f, :, Q_HALF:], lhsT=ident_bf[:], rhs=quads[:, 1, :, Q_HALF:, f, :], start=True, stop=True
                )
                nc.tensor.matmul(
                    places[:, 1, f, :, 0:Q_HALF], lhsT=minus_ident_bf[:], rhs=quads[:, 1, :, 0:Q_HALF, f, :],
                    start=True, stop=True,
                )
            return bank

        def multiply_by_tables(unit, products, bank, f, terms, h0=0, h1=HEADS):
            a, r0, n = unit
            rows = grads[a][:, h0:h1, r0 * HEAD : (r0 + n) * HEAD]
            quads = rows.rearrange("p h (r q f e) -> p h r q f e", r=n, f=2, e=2)[:, :, :, Q_NOPE:, f, :]
            places = products[:, :, f, h0:h1].rearrange("p x h r (q e) -> p x h r q e", e=2)[:, :, :, 0:n]
            tabled = bank[:, :, f].rearrange("p x r (q e) -> p x r q e", e=2)[:, :, r0 : r0 + n]

            for x in terms:
                nc.vector.tensor_tensor(
                    out=places[:, x],
                    in0=quads,
                    in1=tabled[:, x].unsqueeze(1).to_broadcast([P, h1 - h0, n, 2 * Q_HALF, 2]),
                    op=ALU.mult,
                )

        COS, SIN = 0, 1

        def unrotated_of(unit):
            a, r0, n = unit
            gq_rows = wide.tile([P, PARTS, PAIR, K // 2], BF16)
            rows = grads[a][:, :, r0 * HEAD : (r0 + n) * HEAD]
            words = rows.bitcast(F32).rearrange("p h (r q f) -> p h r q f", r=n, f=2)
            places = gq_rows[:].bitcast(F32).rearrange("p f r (h q) -> p f h r q", h=HEADS)
            for f in range(PARTS):
                nc.scalar.copy(out=places[:, f, :, 0:n, 0:Q_NOPE], in_=words[:, :, :, 0:Q_NOPE, f])
            return gq_rows

        def add_terms(engine, n, products, gq_rows, f, h0=0, h1=HEADS):
            places = gq_rows[:].rearrange("p f r (h j) -> p f h r j", h=HEADS)
            engine.tensor_tensor(
                out=places[:, f, h0:h1, 0:n, 2 * Q_NOPE :].rearrange("p h r (j k) -> p h r j k", j=2),
                in0=products[:, 0, f, h0:h1, 0:n].rearrange("p h r (j k) -> p h r j k", j=2),
                in1=products[:, 1, f, h0:h1, 0:n].rearrange("p h r (j k) -> p h r j k", j=2)[:, :, :, ::-1],
                op=ALU.add,
            )

        def turn_tokens(n, gq_rows):
            gq_grouped = stage.tile([P, PASSES, PAIR * P, PACK], BF16, align_bytes=64)
            gq_words = gq_rows[:].bitcast(F32)
            for c in range(PASSES):
                bank = turned.tile([P, 2, n * P], F32, tag="turned")
                for f in range(PARTS):
                    for i in range(n):
                        nc.tensor.transpose(
                            bank[:, f, i * P : (i + 1) * P], gq_words[:, f, i, P * c : P * (c + 1)], ident[:]
                        )
                nc.scalar.copy(
                    out=gq_grouped[:, c, 0 : n * P, :].bitcast(F32), in_=bank[:].rearrange("p f n -> p n f")
                )
            return gq_grouped

        def quantise_tokens(n, gq_grouped, before_last):
            gq_codes = coded.tile([P, PASSES, PAIR * P], U32, align_bytes=64)
            gq_scales = coded.tile([P, PASSES, PAIR * P], U8, align_bytes=64)
            for c in range(PASSES):
                if c == PASSES - 1:
                    before_last()
                nc.vector.quantize_mx(
                    out=gq_codes[:, c, 0 : n * P].bitcast(E5M2X4),
                    scales=gq_scales[:, c, 0 : n * P],
                    in_=gq_grouped[:, c, 0 : n * P, :].rearrange("p s t -> p (s t)"),
                )
            return gq_codes, gq_scales

        w_grouped = keep.tile([P, PASSES, HID, PACK], BF16, align_bytes=64)
        w_codes = keep.tile([P, PASSES, HID], U32, align_bytes=64)
        w_scales = keep.tile([P, PASSES, HID], U8, align_bytes=64)
        w_words = w_rows[:].bitcast(F32)

        def turn_w(q):
            for c in range(PASSES):
                turn(
                    [w_words[:, PAIR * q + j, :] for j in range(PAIR)], c,
                    w_grouped[:, c, PAIR * P * q : PAIR * P * (q + 1), :],
                )

        def quantise_w(half, before_last=lambda: None):
            cols = slice(N_TILE * half, N_TILE * (half + 1))
            for c in range(PASSES):
                if c == PASSES - 1:
                    before_last()
                nc.vector.quantize_mx(
                    out=w_codes[:, c, cols].bitcast(E4M3X4),
                    scales=w_scales[:, c, cols],
                    in_=w_grouped[:, c, cols, :].rearrange("p n t -> p (n t)"),
                )

        def multiply_pass(acc, codes, i, half, c):
            rows = slice(i * P, (i + 1) * P)
            cols = slice(half * N_TILE, (half + 1) * N_TILE)
            nc.tensor.matmul_mx(
                out=acc[:],
                lhsT=codes[0][:, c, rows].bitcast(E5M2X4),
                lhsT_scale=codes[1][:, c, rows],
                rhs=w_codes[:, c, cols].bitcast(E4M3X4),
                rhs_scale=w_scales[:, c, cols],
                start=(c == 0),
                stop=(c == PASSES - 1),
            )

        units = []
        for a in range(CHUNKS):
            units.extend([(a, r, 1) for r in range(PAIR)] if a in (CHUNKS - 2, CHUNKS - 1) else [(a, 0, PAIR)])
        count = len(units)
        last_pair = max([-1] + [u for u in range(count - 1) if units[u][2] == PAIR])
        added_by_vector = (last_pair, count - 1)

        banks = {}
        products_of = {}
        rows_of = {}
        grouped_of = {}
        codes_of = {}
        result_of = {}
        stored = {}

        def tables_for(u):
            if u < count and units[u][0] not in banks:
                banks[units[u][0]] = tables_to_psum(units[u][0])

        def products(u, part, held_back=False):
            if u >= count:
                return
            if part == 0:
                fresh = wide.tile([P, 2, PARTS, HEADS, PAIR, HALF], F32, name="products")
                products_of[u] = fresh
            bank = banks[units[u][0]]
            if u == 0:
                for f in range(PARTS):
                    multiply_by_tables(
                        units[u], products_of[u], bank, f, (COS, SIN),
                        part * HEADS // 2, (part + 1) * HEADS // 2,
                    )
            elif held_back:
                multiply_by_tables(units[u], products_of[u], bank, part, (COS,))
                multiply_by_tables(units[u], products_of[u], bank, part, (SIN,), 1, HEADS)
            else:
                multiply_by_tables(units[u], products_of[u], bank, part, (COS, SIN))

        def rest_of_products(u, part):
            multiply_by_tables(
                units[u], products_of[u], banks[units[u][0]], part, (SIN,), 0, 1
            )

        def add(u, part, engine, h0=0, h1=HEADS):
            if not 0 <= u < count:
                return
            n = units[u][2]
            if u == 0:
                for f in range(PARTS):
                    add_terms(engine, n, products_of[u], rows_of[u], f, part * HEADS // 2, (part + 1) * HEADS // 2)
            else:
                add_terms(engine, n, products_of[u], rows_of[u], part, h0, h1)

        def unrotated(u):
            if u < count:
                rows_of[u] = unrotated_of(units[u])

        def turn_unit(u):
            if 0 <= u < count:
                grouped_of[u] = turn_tokens(units[u][2], rows_of[u])

        def quantise_unit(u, before_last=lambda: None):
            if 0 <= u < count:
                codes_of[u] = quantise_tokens(units[u][2], grouped_of[u], before_last)

        def tiles_of(u):
            return [(u, i, half) for i in range(units[u][2]) for half in range(N_HALVES)] if 0 <= u < count else []

        def multiply(jobs):
            for u, i, half in jobs:
                a, r0, n = units[u]
                if u not in result_of:
                    fresh = results.tile([P, PAIR, HID], F32, name="result")
                    result_of[u] = fresh
                    stored[u] = 0
                acc = sums.tile([P, N_TILE], F32)
                for c in range(PASSES):
                    multiply_pass(acc, codes_of[u], i, half, c)
                nc.scalar.copy(out=result_of[u][:, i, half * N_TILE : (half + 1) * N_TILE], in_=acc[:])
                stored[u] += 1
                if u == last_pair and stored[u] % N_HALVES == 0:
                    nc.sync.dma_start(out=out_rows[a][:, i, :], in_=result_of[u][:, i, :])
                elif u != last_pair and stored[u] == n * N_HALVES:
                    nc.sync.dma_start(out=out_rows[a][:, r0 : r0 + n, :], in_=result_of[u][:, 0:n, :])

        def multiply_last():
            u = count - 1
            a, r0, n = units[u]
            result = results.tile([P, PAIR, HID], F32, name="result")
            accs = []
            for half in range(N_HALVES):
                acc = sums.tile([P, N_TILE], F32)
                accs.append(acc)
            for c in range(PASSES):
                for half in range(N_HALVES):
                    multiply_pass(accs[half], codes_of[u], 0, half, c)
            for half, copy in enumerate((nc.scalar.copy, nc.vector.tensor_copy)):
                cols = slice(half * N_TILE, (half + 1) * N_TILE)
                copy(out=result[:, 0, cols], in_=accs[half][:])
                nc.sync.dma_start(out=out_rows[a][:, r0, cols], in_=result[:, 0, cols])

        runs = {s: (tiles_of(s - 2)[0:2], tiles_of(s - 2)[2:]) for s in range(count + 1)}
        half = {u: len(tiles_of(u)) // 2 for u in range(count)}
        runs = {}
        for s in range(count):
            first = tiles_of(s - 3)[half[s - 3]:] if s >= 5 else []
            second = tiles_of(s - 2)[0:half[s - 2]] if s >= 4 else []
            if s == count - 1:
                second = tiles_of(s - 2)[0:3]
            runs[s] = (first, second)
        runs[2] = ([], [(0, 0, 0), (0, 1, 0)])
        runs[3] = ([], [(1, 0, 0), (1, 1, 0), (0, 0, 1), (0, 1, 1)])
        runs[4] = ([(1, 0, 1), (1, 1, 1)], runs[4][1])
        tables_for(0)
        tables_for(1)
        unrotated(0)
        for s in range(count):
            mid = s >= 2
            products(s, 0, mid)
            if s >= 1 and s - 1 not in added_by_vector:
                add(s - 1, 1, nc.gpsimd, 0, 6 if 3 <= s <= 5 else HEADS)
            if 3 <= s <= 5:
                add(s - 1, 1, nc.vector, 6, HEADS)
            if s == 2:
                quantise_unit(0)
                quantise_w(0)
            if s == 3:
                quantise_unit(1)
                quantise_w(1, lambda: rest_of_products(3, 0))
            if s >= 4:
                quantise_unit(s - 2, lambda: rest_of_products(s, 0))
            if s == 2:
                rest_of_products(s, 0)
            multiply(runs[s][0])
            tables_for(s + 1)
            hold = False
            products(s, 1, hold)
            add(s, 0, nc.gpsimd)
            if s == 0:
                unrotated(1)
                turn_w(0)
            if s not in (99,):
                turn_unit(s - 1)
            if s == 1:
                turn_w(1)
                turn_w(2)
            if s == 2:
                turn_w(3)
            if s >= 1:
                unrotated(s + 1)
            multiply(runs[s][1])
            if s == count - 1:
                add(s, 1, nc.vector)
            if s == count - 1:
                quantise_unit(s - 1)
            if hold:
                rest_of_products(s, 1)
            if s == last_pair:
                add(s, 1, nc.vector)
        turn_unit(count - 1)
        multiply(tiles_of(count - 3)[3:] + tiles_of(count - 2))
        quantise_unit(count - 1)
        multiply_last()
